import numpy as np
import ml_dtypes


def mxq(x, axis, fmt="e4m3"):
    dtype, down = {"e4m3": (ml_dtypes.float8_e4m3fn, 7), "e5m2": (ml_dtypes.float8_e5m2, 14)}[fmt]
    v = np.moveaxis(np.asarray(x, np.float32).astype(ml_dtypes.bfloat16).astype(np.float64), axis, -1)
    blocks = v.reshape(v.shape[:-1] + (-1, 32))
    amax = np.abs(blocks).max(-1, keepdims=True)
    byte = np.maximum(np.where(amax > 0, np.frexp(amax)[1] - 1 + 127, 0) - down, 1)
    scale = np.exp2(byte - 127.0)
    codes = (blocks / scale).astype(np.float32).astype(dtype).astype(np.float64)
    return np.moveaxis((codes * scale).reshape(v.shape), -1, axis)


WIDE = False


def mx_kscale(k):
    if not WIDE:
        return np.ones(k)
    levels = np.array([10, -10, 5, -5, 0])
    if k % 512:
        return np.exp2(np.random.permutation(np.resize(levels, k // 32))).repeat(32)
    a = np.empty((k // 512, 16))
    for p in range(k // 512):
        a[p, :8] = np.random.permutation(np.resize(levels, 8))
        for g in range(8):
            far = levels[np.abs(levels - a[p, g]) >= 10]
            a[p, g + 8] = far[np.random.randint(len(far))]
    return np.exp2(a.ravel()).repeat(32)


BF16 = ml_dtypes.bfloat16


def bf(x):
    return np.asarray(x, np.float32).astype(BF16)


def f64(x):
    return np.asarray(x).astype(np.float64)


N, K, D_IN, HC, H = 256, 8, 1024, 1024, 1024


def sigmoid(v):
    return 1.0 / (1.0 + np.exp(-v))


def setup_inputs():
    s, t = mx_kscale(D_IN), mx_kscale(HC)
    return {
        "x": bf(np.random.standard_normal((N, D_IN)) * s),
        "child_h": bf(np.random.standard_normal((N, K, HC)) * t),
        "child_c": bf(np.random.standard_normal((N, K, H)) * 0.5),
        "Wf": bf(np.random.standard_normal((D_IN, H)) * 0.7 / np.sqrt(D_IN) / s[:, None]),
        "bWf": bf(np.random.standard_normal(H) * 0.3),
        "Uf": bf(np.random.standard_normal((HC, H)) * 0.7 / np.sqrt(HC) / t[:, None]),
        "bUf": bf(np.random.standard_normal(H) * 0.3),
    }


def reference(x, child_h, child_c, Wf, bWf, Uf, bUf):
    xf = (mxq(f64(x), 1, "e4m3") @ mxq(f64(Wf), 0, "e4m3")) + f64(bWf)
    hf = mxq(f64(child_h), 2, "e4m3") @ mxq(f64(Uf), 0, "e4m3")
    f = sigmoid(xf[:, None, :] + hf + f64(bUf))
    return (f * f64(child_c)).sum(axis=1)

@@ -1,0 +1,239 @@
+from contextlib import ExitStack
+
+import concourse.mybir as mybir
+from concourse.masks import make_identity
+
+F32 = mybir.dt.float32
+BF16 = mybir.dt.bfloat16
+U32 = mybir.dt.uint32
+U8 = mybir.dt.uint8
+FP8X4 = mybir.dt.float8_e4m3fn_x4
+ADD = mybir.AluOpType.add
+MULT = mybir.AluOpType.mult
+SIGMOID = mybir.ActivationFunctionType.Sigmoid
+
+P = 128
+NODES = 256
+CHILDREN = 8
+D = 1024
+H = 1024
+PACK = 4
+K_PASS = P * PACK
+PASSES = D // K_PASS
+PAIR_ROWS = K_PASS // 2
+N_TILE = 512
+H_HALVES = H // N_TILE
+NODE_BLOCKS = NODES // P
+BLOCKS = N_TILE // P
+
+FLOPS = 2 * (NODES + NODES * CHILDREN) * D * H
+VECTOR_COLS = 256
+AHEAD = 6
+
+
+def load_weight_half(nc, pool, w, cols):
+    raw = pool.tile([P, PASSES, PACK, N_TILE], BF16, name="w_raw")
+    for g in range(PASSES):
+        nc.sync.dma_start(
+            out=raw[:, g],
+            in_=w[K_PASS * g : K_PASS * (g + 1), cols].rearrange("(p t) c -> p t c", t=PACK),
+        )
+    return raw
+
+
+def quantise_weight_pass(nc, stage, raw_pass, codes, scales):
+    grouped = stage.tile([P, N_TILE, PACK], BF16, name="w_grouped", align_bytes=64)
+    nc.vector.tensor_copy(
+        out=grouped[:, :VECTOR_COLS, :].rearrange("p (c i) t -> p c t i", i=4),
+        in_=raw_pass[:, :, :VECTOR_COLS].rearrange("p t (c i) -> p c t i", i=4),
+    )
+    nc.scalar.copy(
+        out=grouped[:, VECTOR_COLS:, :].rearrange("p (c i) t -> p c t i", i=4),
+        in_=raw_pass[:, :, VECTOR_COLS:].rearrange("p t (c i) -> p c t i", i=4),
+    )
+    nc.vector.quantize_mx(
+        out=codes.bitcast(FP8X4),
+        scales=scales,
+        in_=grouped[:].rearrange("p c t -> p (c t)"),
+    )
+
+
+def transpose_and_quantise(nc, psum, stage, words, ident, codes, scales):
+    turned = psum.tile([P, PASSES, 2, P], F32, name="turned")
+    for g in range(PASSES):
+        for u in range(2):
+            nc.tensor.transpose(turned[:, g, u, :], words[:, PAIR_ROWS * g + u : PAIR_ROWS * (g + 1) : 2], ident[:])
+    grouped = stage.tile([P, PASSES * P * PACK], BF16, name="a_grouped", align_bytes=64)
+    nc.scalar.copy(
+        out=grouped[:].bitcast(F32).rearrange("p (g r u) -> p g r u", g=PASSES, u=2),
+        in_=turned[:].rearrange("p g u r -> p g r u"),
+    )
+    nc.vector.quantize_mx(
+        out=codes.rearrange("p g r -> p (g r)").bitcast(FP8X4),
+        scales=scales.rearrange("p g r -> p (g r)"),
+        in_=grouped[:],
+    )
+
+
+def mx_product(nc, acc, a_codes, a_scales, w_codes, w_scales):
+    for g in range(PASSES):
+        nc.tensor.matmul_mx(
+            out=acc,
+            lhsT=a_codes[:, g, :].bitcast(FP8X4),
+            lhsT_scale=a_scales[:, g, :],
+            rhs=w_codes[:, g, :].bitcast(FP8X4),
+            rhs_scale=w_scales[:, g, :],
+            start=(g == 0),
+            stop=(g == PASSES - 1),
+        )
+
+
+def tile_childsumtreelstmcell_pa_kernel(tc, x, child_h, child_c, Wf, bWf, Uf, bUf, out):
+    nc = tc.nc
+    with ExitStack() as stack:
+        const = stack.enter_context(tc.tile_pool(name="const", bufs=1))
+        inputs = stack.enter_context(tc.tile_pool(name="inputs", bufs=1))
+        raws = stack.enter_context(tc.tile_pool(name="raws", bufs=2 * H_HALVES))
+        cells = stack.enter_context(tc.tile_pool(name="cells", bufs=H_HALVES * NODE_BLOCKS))
+        keep = stack.enter_context(tc.tile_pool(name="keep", bufs=1))
+        stage = stack.enter_context(tc.tile_pool(name="stage", bufs=3))
+        work = stack.enter_context(tc.tile_pool(name="work", bufs=4))
+        psum_turn = stack.enter_context(tc.psum_pool(name="psum_turn", bufs=2))
+        psum_acc = stack.enter_context(tc.psum_pool(name="psum_acc", bufs=3))
+        psum_sum = stack.enter_context(tc.psum_pool(name="psum_sum", bufs=2))
+        psum_back = stack.enter_context(tc.psum_pool(name="psum_back", bufs=1))
+
+        halves = [slice(N_TILE * hh, N_TILE * (hh + 1)) for hh in range(H_HALVES)]
+        node_rows = [slice(P * nb, P * (nb + 1)) for nb in range(NODE_BLOCKS)]
+
+        ident = const.tile([P, P], F32, name="ident")
+        make_identity(nc, ident[:])
+        ones = const.tile([P, P], BF16, name="ones")
+        nc.vector.memset(ones[:], 1.0)
+        bias_rows = const.tile([P, H], BF16, name="bias_rows")
+        nc.vector.memset(bias_rows[:], 0.0)
+        warm = const.tile([P, 1], F32, name="warm")
+        nc.scalar.activation(out=warm[:], in_=ones[:, 0:1], func=SIGMOID)
+
+        x_sb = inputs.tile([P, NODE_BLOCKS * D], BF16, name="x_sb")
+        h_sb = [inputs.tile([P, CHILDREN * D], BF16, name="h_sb%d" % nb) for nb in range(NODE_BLOCKS)]
+        w_raw = {}
+        c_sb = {}
+
+        def load_children(nb, part):
+            kids = slice(CHILDREN // 2 * part, CHILDREN // 2 * (part + 1))
+            nc.sync.dma_start(
+                out=h_sb[nb][:].rearrange("p (k d) -> p k d", k=CHILDREN)[:, kids, :],
+                in_=child_h[node_rows[nb], kids, :],
+            )
+
+        def load_cells(hh, nb, part):
+            kids = slice(CHILDREN // 2 * part, CHILDREN // 2 * (part + 1))
+            if part == 0:
+                c_sb[hh, nb] = cells.tile([P, CHILDREN, N_TILE], BF16, name="c_sb")
+            nc.sync.dma_start(out=c_sb[hh, nb][:, kids, :], in_=child_c[node_rows[nb], kids, halves[hh]])
+
+        nc.sync.dma_start(
+            out=x_sb[:].rearrange("p (b d) -> p b d", b=NODE_BLOCKS),
+            in_=x.rearrange("(b p) d -> p b d", p=P),
+        )
+        nc.sync.dma_start(out=bias_rows[0:1, :], in_=bWf.unsqueeze(0))
+        nc.sync.dma_start(out=bias_rows[1:2, :], in_=bUf.unsqueeze(0))
+        w_raw["wf", 0] = load_weight_half(nc, raws, Wf, halves[0])
+        load_children(0, 0)
+        w_raw["uf", 0] = load_weight_half(nc, raws, Uf, halves[0])
+        load_children(0, 1)
+        load_cells(0, 0, 0)
+        load_children(1, 0)
+        load_cells(0, 0, 1)
+        w_raw["wf", 1] = load_weight_half(nc, raws, Wf, halves[1])
+        load_children(1, 1)
+        load_cells(0, 1, 0)
+        w_raw["uf", 1] = load_weight_half(nc, raws, Uf, halves[1])
+        load_cells(0, 1, 1)
+        for nb in range(NODE_BLOCKS):
+            for part in range(2):
+                load_cells(1, nb, part)
+
+        w_codes = {}
+        w_scales = {}
+        for name in ("wf", "uf"):
+            w_codes[name] = keep.tile([P, H_HALVES, PASSES, N_TILE], U32, name=name + "_codes", align_bytes=64)
+            w_scales[name] = keep.tile([P, H_HALVES, PASSES, N_TILE], U8, name=name + "_scales", align_bytes=64)
+        x_codes = keep.tile([P, NODE_BLOCKS, PASSES, P], U32, name="x_codes", align_bytes=64)
+        x_scales = keep.tile([P, NODE_BLOCKS, PASSES, P], U8, name="x_scales", align_bytes=64)
+        h_codes = keep.tile([P, NODE_BLOCKS, CHILDREN, PASSES, P], U32, name="h_codes", align_bytes=64)
+        h_scales = keep.tile([P, NODE_BLOCKS, CHILDREN, PASSES, P], U8, name="h_scales", align_bytes=64)
+
+        def prepare_weight_pass(name, hh, g):
+            quantise_weight_pass(nc, stage, w_raw[name, hh][:, g], w_codes[name][:, hh, g, :], w_scales[name][:, hh, g, :])
+
+        words_per_row = D // 2
+
+        def prepare_child(nb, k):
+            words = h_sb[nb][:].bitcast(F32)[:, words_per_row * k : words_per_row * (k + 1)]
+            transpose_and_quantise(nc, psum_turn, stage, words, ident, h_codes[:, nb, k], h_scales[:, nb, k])
+
+        bias_sb = keep.tile([P, H], F32, name="bias_sb")
+        for hh in range(H_HALVES):
+            bias_ps = psum_acc.tile([P, N_TILE], F32, name="acc")
+            nc.tensor.matmul(out=bias_ps[:], lhsT=ones[:], rhs=bias_rows[:, halves[hh]], start=True, stop=True)
+            nc.scalar.copy(out=bias_sb[:, halves[hh]], in_=bias_ps[:])
+
+        for nb in range(NODE_BLOCKS):
+            words = x_sb[:].bitcast(F32)[:, words_per_row * nb : words_per_row * (nb + 1)]
+            transpose_and_quantise(nc, psum_turn, stage, words, ident, x_codes[:, nb], x_scales[:, nb])
+        for name in ("wf", "uf"):
+            for g in range(PASSES):
+                prepare_weight_pass(name, 0, g)
+        for k in range(AHEAD):
+            prepare_child(0, k)
+
+        xfb = keep.tile([P, NODE_BLOCKS, H], F32, name="xfb")
+        summed_t = None
+
+        for step in range(H_HALVES * NODE_BLOCKS * CHILDREN):
+            hh = step // (NODE_BLOCKS * CHILDREN)
+            nb = step // CHILDREN % NODE_BLOCKS
+            k = step % CHILDREN
+
+            if k == 0:
+                xf_ps = psum_acc.tile([P, N_TILE], F32, name="acc")
+                mx_product(nc, xf_ps[:], x_codes[:, nb], x_scales[:, nb], w_codes["wf"][:, hh], w_scales["wf"][:, hh])
+                nc.vector.tensor_tensor(out=xfb[:, nb, halves[hh]], in0=xf_ps[:], in1=bias_sb[:, halves[hh]], op=ADD)
+                summed_t = psum_sum.tile([P, BLOCKS, P], F32, name="summed_t")
+
+            hf_ps = psum_acc.tile([P, N_TILE], F32, name="acc")
+            mx_product(nc, hf_ps[:], h_codes[:, nb, k], h_scales[:, nb, k], w_codes["uf"][:, hh], w_scales["uf"][:, hh])
+            z = work.tile([P, N_TILE], F32, name="z")
+            nc.vector.tensor_tensor(out=z[:], in0=hf_ps[:], in1=xfb[:, nb, halves[hh]], op=ADD)
+            gate = work.tile([P, N_TILE], F32, name="gate")
+            nc.scalar.activation(out=gate[:], in_=z[:], func=SIGMOID)
+            weighted = work.tile([P, N_TILE], F32, name="weighted")
+            nc.vector.tensor_tensor(out=weighted[:], in0=gate[:], in1=c_sb[hh, nb][:, k, :], op=MULT)
+
+            for j in range(BLOCKS):
+                nc.tensor.matmul(
+                    out=summed_t[:, j, :],
+                    lhsT=weighted[:, P * j : P * (j + 1)],
+                    rhs=ident[:],
+                    is_transpose=True,
+                    start=(k == 0 and j == 0),
+                    stop=(k == CHILDREN - 1 and j == BLOCKS - 1),
+                )
+
+            if k == CHILDREN - 1:
+                summed_t_sb = work.tile([P, BLOCKS, P], F32, name="summed_t_sb")
+                nc.scalar.copy(out=summed_t_sb[:], in_=summed_t[:])
+                result_ps = psum_back.tile([P, N_TILE], F32, name="result_ps")
+                for j in range(BLOCKS):
+                    nc.tensor.transpose(result_ps[:, P * j : P * (j + 1)], summed_t_sb[:, j, :], ident[:])
+                result = work.tile([P, N_TILE], F32, name="result")
+                nc.scalar.copy(out=result[:], in_=result_ps[:])
+                nc.sync.dma_start(out=out[node_rows[nb], halves[hh]], in_=result[:])
+
+            child = step + AHEAD
+            if child < NODE_BLOCKS * CHILDREN:
+                prepare_child(child // CHILDREN, child % CHILDREN)
+            if hh == 0 and step % 4 == 3:
+                prepare_weight_pass(("wf", "uf")[step // 8], 1, step // 4 % PASSES)

@@ -11,6 +11,7 @@ FP8X4 = mybir.dt.float8_e4m3fn_x4
 ADD = mybir.AluOpType.add
 MULT = mybir.AluOpType.mult
 SIGMOID = mybir.ActivationFunctionType.Sigmoid
+IDENTITY = mybir.ActivationFunctionType.Identity
 
 P = 128
 NODES = 256
@@ -20,72 +21,15 @@ H = 1024
 PACK = 4
 K_PASS = P * PACK
 PASSES = D // K_PASS
-PAIR_ROWS = K_PASS // 2
-N_TILE = 512
-H_HALVES = H // N_TILE
+PASS_WORDS = K_PASS // 2
 NODE_BLOCKS = NODES // P
-BLOCKS = N_TILE // P
+PART = 4
+PARTS = CHILDREN // PART
+N_TILE = PART * P
+PAIR = 2 * P
+COL_PAIRS = H // PAIR
 
 FLOPS = 2 * (NODES + NODES * CHILDREN) * D * H
-VECTOR_COLS = 256
-AHEAD = 6
-
-
-def load_weight_half(nc, pool, w, cols):
-    raw = pool.tile([P, PASSES, PACK, N_TILE], BF16, name="w_raw")
-    for g in range(PASSES):
-        nc.sync.dma_start(
-            out=raw[:, g],
-            in_=w[K_PASS * g : K_PASS * (g + 1), cols].rearrange("(p t) c -> p t c", t=PACK),
-        )
-    return raw
-
-
-def quantise_weight_pass(nc, stage, raw_pass, codes, scales):
-    grouped = stage.tile([P, N_TILE, PACK], BF16, name="w_grouped", align_bytes=64)
-    nc.vector.tensor_copy(
-        out=grouped[:, :VECTOR_COLS, :].rearrange("p (c i) t -> p c t i", i=4),
-        in_=raw_pass[:, :, :VECTOR_COLS].rearrange("p t (c i) -> p c t i", i=4),
-    )
-    nc.scalar.copy(
-        out=grouped[:, VECTOR_COLS:, :].rearrange("p (c i) t -> p c t i", i=4),
-        in_=raw_pass[:, :, VECTOR_COLS:].rearrange("p t (c i) -> p c t i", i=4),
-    )
-    nc.vector.quantize_mx(
-        out=codes.bitcast(FP8X4),
-        scales=scales,
-        in_=grouped[:].rearrange("p c t -> p (c t)"),
-    )
-
-
-def transpose_and_quantise(nc, psum, stage, words, ident, codes, scales):
-    turned = psum.tile([P, PASSES, 2, P], F32, name="turned")
-    for g in range(PASSES):
-        for u in range(2):
-            nc.tensor.transpose(turned[:, g, u, :], words[:, PAIR_ROWS * g + u : PAIR_ROWS * (g + 1) : 2], ident[:])
-    grouped = stage.tile([P, PASSES * P * PACK], BF16, name="a_grouped", align_bytes=64)
-    nc.scalar.copy(
-        out=grouped[:].bitcast(F32).rearrange("p (g r u) -> p g r u", g=PASSES, u=2),
-        in_=turned[:].rearrange("p g u r -> p g r u"),
-    )
-    nc.vector.quantize_mx(
-        out=codes.rearrange("p g r -> p (g r)").bitcast(FP8X4),
-        scales=scales.rearrange("p g r -> p (g r)"),
-        in_=grouped[:],
-    )
-
-
-def mx_product(nc, acc, a_codes, a_scales, w_codes, w_scales):
-    for g in range(PASSES):
-        nc.tensor.matmul_mx(
-            out=acc,
-            lhsT=a_codes[:, g, :].bitcast(FP8X4),
-            lhsT_scale=a_scales[:, g, :],
-            rhs=w_codes[:, g, :].bitcast(FP8X4),
-            rhs_scale=w_scales[:, g, :],
-            start=(g == 0),
-            stop=(g == PASSES - 1),
-        )
 
 
 def tile_childsumtreelstmcell_pa_kernel(tc, x, child_h, child_c, Wf, bWf, Uf, bUf, out):
@@ -93,147 +37,318 @@ def tile_childsumtreelstmcell_pa_kernel(tc, x, child_h, child_c, Wf, bWf, Uf, bU
     with ExitStack() as stack:
         const = stack.enter_context(tc.tile_pool(name="const", bufs=1))
         inputs = stack.enter_context(tc.tile_pool(name="inputs", bufs=1))
-        raws = stack.enter_context(tc.tile_pool(name="raws", bufs=2 * H_HALVES))
-        cells = stack.enter_context(tc.tile_pool(name="cells", bufs=H_HALVES * NODE_BLOCKS))
         keep = stack.enter_context(tc.tile_pool(name="keep", bufs=1))
         stage = stack.enter_context(tc.tile_pool(name="stage", bufs=3))
-        work = stack.enter_context(tc.tile_pool(name="work", bufs=4))
+        work = stack.enter_context(tc.tile_pool(name="work", bufs=3))
         psum_turn = stack.enter_context(tc.psum_pool(name="psum_turn", bufs=2))
         psum_acc = stack.enter_context(tc.psum_pool(name="psum_acc", bufs=3))
-        psum_sum = stack.enter_context(tc.psum_pool(name="psum_sum", bufs=2))
-        psum_back = stack.enter_context(tc.psum_pool(name="psum_back", bufs=1))
+        psum_cell = stack.enter_context(tc.psum_pool(name="psum_cell", bufs=2))
+        psum_sum = stack.enter_context(tc.psum_pool(name="psum_sum", bufs=1))
 
-        halves = [slice(N_TILE * hh, N_TILE * (hh + 1)) for hh in range(H_HALVES)]
+        stack.enter_context(tc.manual_schedule())
+
         node_rows = [slice(P * nb, P * (nb + 1)) for nb in range(NODE_BLOCKS)]
 
         ident = const.tile([P, P], F32, name="ident")
         make_identity(nc, ident[:])
-        ones = const.tile([P, P], BF16, name="ones")
-        nc.vector.memset(ones[:], 1.0)
-        bias_rows = const.tile([P, H], BF16, name="bias_rows")
+        bias_rows = const.tile([P, PAIR], BF16, name="bias_rows")
         nc.vector.memset(bias_rows[:], 0.0)
         warm = const.tile([P, 1], F32, name="warm")
-        nc.scalar.activation(out=warm[:], in_=ones[:, 0:1], func=SIGMOID)
+        nc.scalar.activation(out=warm[:], in_=ident[:, 0:1], func=SIGMOID)
 
         x_sb = inputs.tile([P, NODE_BLOCKS * D], BF16, name="x_sb")
-        h_sb = [inputs.tile([P, CHILDREN * D], BF16, name="h_sb%d" % nb) for nb in range(NODE_BLOCKS)]
-        w_raw = {}
+        h_sb = {}
         c_sb = {}
+        w_raw = {}
 
-        def load_children(nb, part):
-            kids = slice(CHILDREN // 2 * part, CHILDREN // 2 * (part + 1))
+        def load_weight(name, w, jj, count):
+            first, width = PAIR * jj, PAIR * count
+            for g in range(PASSES):
+                raw = inputs.tile([P, PACK, width], BF16, name="%s_raw%d%d" % (name, jj, g))
+                nc.sync.dma_start(
+                    out=raw[:],
+                    in_=w[K_PASS * g : K_PASS * (g + 1), first : first + width].rearrange("(p t) c -> p t c", t=PACK),
+                )
+                for i in range(count):
+                    w_raw[name, jj + i, g] = raw[:, :, PAIR * i : PAIR * (i + 1)]
+
+        def load_children(nb, kh, first, count):
+            if first == 0:
+                h_sb[nb, kh] = inputs.tile([P, PART * D], BF16, name="h_sb%d%d" % (nb, kh))
+            kids = slice(PART * kh + first, PART * kh + first + count)
             nc.sync.dma_start(
-                out=h_sb[nb][:].rearrange("p (k d) -> p k d", k=CHILDREN)[:, kids, :],
+                out=h_sb[nb, kh][:].rearrange("p (k d) -> p k d", k=PART)[:, first : first + count, :],
                 in_=child_h[node_rows[nb], kids, :],
             )
 
-        def load_cells(hh, nb, part):
-            kids = slice(CHILDREN // 2 * part, CHILDREN // 2 * (part + 1))
-            if part == 0:
-                c_sb[hh, nb] = cells.tile([P, CHILDREN, N_TILE], BF16, name="c_sb")
-            nc.sync.dma_start(out=c_sb[hh, nb][:, kids, :], in_=child_c[node_rows[nb], kids, halves[hh]])
+        def load_cells(nb, kh, half):
+            c_sb[nb, kh, half] = inputs.tile([P, PART * 2 * PAIR], BF16, name="c_sb%d%d%d" % (nb, kh, half))
+            nc.sync.dma_start(
+                out=c_sb[nb, kh, half][:].rearrange("p (k c) -> p k c", k=PART),
+                in_=child_c[node_rows[nb], PART * kh : PART * (kh + 1), 2 * PAIR * half : 2 * PAIR * (half + 1)],
+            )
 
         nc.sync.dma_start(
             out=x_sb[:].rearrange("p (b d) -> p b d", b=NODE_BLOCKS),
             in_=x.rearrange("(b p) d -> p b d", p=P),
         )
-        nc.sync.dma_start(out=bias_rows[0:1, :], in_=bWf.unsqueeze(0))
-        nc.sync.dma_start(out=bias_rows[1:2, :], in_=bUf.unsqueeze(0))
-        w_raw["wf", 0] = load_weight_half(nc, raws, Wf, halves[0])
-        load_children(0, 0)
-        w_raw["uf", 0] = load_weight_half(nc, raws, Uf, halves[0])
-        load_children(0, 1)
+        for row, vec in ((0, bWf), (COL_PAIRS, bUf)):
+            nc.sync.dma_start(out=bias_rows[row : row + COL_PAIRS, :], in_=vec.rearrange("(j c) -> j c", c=PAIR))
+        load_weight("wf", Wf, 0, 1)
+        load_children(0, 0, 0, 2)
+        load_weight("uf", Uf, 0, 1)
+        load_children(0, 0, 2, 2)
+        load_children(0, 1, 0, 4)
         load_cells(0, 0, 0)
-        load_children(1, 0)
-        load_cells(0, 0, 1)
-        w_raw["wf", 1] = load_weight_half(nc, raws, Wf, halves[1])
-        load_children(1, 1)
+        load_children(1, 0, 0, 4)
+        load_weight("wf", Wf, 1, 1)
         load_cells(0, 1, 0)
-        w_raw["uf", 1] = load_weight_half(nc, raws, Uf, halves[1])
-        load_cells(0, 1, 1)
+        load_weight("uf", Uf, 1, 1)
+        load_children(1, 1, 0, 4)
+        load_cells(1, 0, 0)
+        load_cells(1, 1, 0)
+        load_weight("wf", Wf, 2, 2)
+        load_weight("uf", Uf, 2, 2)
         for nb in range(NODE_BLOCKS):
-            for part in range(2):
-                load_cells(1, nb, part)
+            for kh in range(PARTS):
+                load_cells(nb, kh, 1)
 
         w_codes = {}
         w_scales = {}
         for name in ("wf", "uf"):
-            w_codes[name] = keep.tile([P, H_HALVES, PASSES, N_TILE], U32, name=name + "_codes", align_bytes=64)
-            w_scales[name] = keep.tile([P, H_HALVES, PASSES, N_TILE], U8, name=name + "_scales", align_bytes=64)
-        x_codes = keep.tile([P, NODE_BLOCKS, PASSES, P], U32, name="x_codes", align_bytes=64)
-        x_scales = keep.tile([P, NODE_BLOCKS, PASSES, P], U8, name="x_scales", align_bytes=64)
-        h_codes = keep.tile([P, NODE_BLOCKS, CHILDREN, PASSES, P], U32, name="h_codes", align_bytes=64)
-        h_scales = keep.tile([P, NODE_BLOCKS, CHILDREN, PASSES, P], U8, name="h_scales", align_bytes=64)
+            w_codes[name] = keep.tile([P, PASSES, COL_PAIRS, PAIR], U32, name=name + "_codes", align_bytes=64)
+            w_scales[name] = keep.tile([P, PASSES, COL_PAIRS, PAIR], U8, name=name + "_scales", align_bytes=64)
+        x_codes = keep.tile([P, PASSES, NODES], U32, name="x_codes", align_bytes=64)
+        x_scales = keep.tile([P, PASSES, NODES], U8, name="x_scales", align_bytes=64)
+        h_codes = keep.tile([P, NODE_BLOCKS, PARTS, PASSES, N_TILE], U32, name="h_codes", align_bytes=64)
+        h_scales = keep.tile([P, NODE_BLOCKS, PARTS, PASSES, N_TILE], U8, name="h_scales", align_bytes=64)
 
-        def prepare_weight_pass(name, hh, g):
-            quantise_weight_pass(nc, stage, w_raw[name, hh][:, g], w_codes[name][:, hh, g, :], w_scales[name][:, hh, g, :])
+        def turn_rows(words, first_row, g, grouped):
+            turned = psum_turn.tile([P, 2, 2, P], F32, name="turned")
+            for r in range(2):
+                start = D // 2 * (first_row + r) + PASS_WORDS * g
+                for u in range(2):
+                    nc.tensor.transpose(turned[:, r, u, :], words[:, start + u : start + PASS_WORDS : 2], ident[:])
+            nc.scalar.copy(
+                out=grouped.bitcast(F32).rearrange("p (r n u) -> p r n u", r=2, u=2),
+                in_=turned[:].rearrange("p r u n -> p r n u"),
+            )
 
-        words_per_row = D // 2
+        grouped = {}
 
-        def prepare_child(nb, k):
-            words = h_sb[nb][:].bitcast(F32)[:, words_per_row * k : words_per_row * (k + 1)]
-            transpose_and_quantise(nc, psum_turn, stage, words, ident, h_codes[:, nb, k], h_scales[:, nb, k])
+        def turn_x(g):
+            grouped["x", g] = stage.tile([P, NODES * PACK], BF16, name="x_grouped", align_bytes=64)
+            turn_rows(x_sb[:].bitcast(F32), 0, g, grouped["x", g][:])
 
-        bias_sb = keep.tile([P, H], F32, name="bias_sb")
-        for hh in range(H_HALVES):
-            bias_ps = psum_acc.tile([P, N_TILE], F32, name="acc")
-            nc.tensor.matmul(out=bias_ps[:], lhsT=ones[:], rhs=bias_rows[:, halves[hh]], start=True, stop=True)
-            nc.scalar.copy(out=bias_sb[:, halves[hh]], in_=bias_ps[:])
+        def quantise_x(g):
+            nc.vector.quantize_mx(
+                out=x_codes[:, g, :].bitcast(FP8X4), scales=x_scales[:, g, :], in_=grouped["x", g][:]
+            )
 
-        for nb in range(NODE_BLOCKS):
-            words = x_sb[:].bitcast(F32)[:, words_per_row * nb : words_per_row * (nb + 1)]
-            transpose_and_quantise(nc, psum_turn, stage, words, ident, x_codes[:, nb], x_scales[:, nb])
-        for name in ("wf", "uf"):
+        def turn_children(n, g, half):
+            if half == 0:
+                grouped[n, g] = stage.tile([P, N_TILE * PACK], BF16, name="h_grouped", align_bytes=64)
+            size = N_TILE * PACK // 2
+            turn_rows(
+                h_sb[n // PARTS, n % PARTS][:].bitcast(F32), 2 * half, g, grouped[n, g][:, size * half : size * (half + 1)]
+            )
+
+        def quantise_children(n, g):
+            nb, kh = n // PARTS, n % PARTS
+            nc.vector.quantize_mx(
+                out=h_codes[:, nb, kh, g, :].bitcast(FP8X4), scales=h_scales[:, nb, kh, g, :], in_=grouped[n, g][:]
+            )
+
+        def group_weight(name, jj, g, copy):
+            grouped[name, jj, g] = stage.tile([P, 2, P, PACK], BF16, name="w_grouped", align_bytes=64)
+            copy(out=grouped[name, jj, g][:], in_=w_raw[name, jj, g].rearrange("p t (w e) -> p e w t", e=2))
+
+        def quantise_weight(name, jj, g):
+            nc.vector.quantize_mx(
+                out=w_codes[name][:, g, jj, :].bitcast(FP8X4),
+                scales=w_scales[name][:, g, jj, :],
+                in_=grouped[name, jj, g][:].rearrange("p e w t -> p (e w t)"),
+            )
+
+        bias = keep.tile([P, 2 * COL_PAIRS], F32, name="bias")
+
+        def prepare_bias():
+            turned = psum_turn.tile([P, 2, 2, P], F32, name="turned")
+            nc.tensor.transpose(turned[:, 0, 0, :], bias_rows[:].bitcast(F32), ident[:])
+            pairs = keep.tile([P, 2 * COL_PAIRS], F32, name="bias_pairs")
+            nc.scalar.copy(out=pairs[:], in_=turned[:, 0, 0, 0 : 2 * COL_PAIRS])
+            both = pairs[:].bitcast(BF16)
+            nc.vector.tensor_tensor(
+                out=bias[:], in0=both[:, 0 : 2 * COL_PAIRS], in1=both[:, 2 * COL_PAIRS : 4 * COL_PAIRS], op=ADD
+            )
+
+        xfb = keep.tile([P, COL_PAIRS, 2, NODES], F32, name="xfb")
+
+        def product(acc, name, jj, e, codes, scales):
+            cols = slice(P * e, P * (e + 1))
             for g in range(PASSES):
-                prepare_weight_pass(name, 0, g)
-        for k in range(AHEAD):
-            prepare_child(0, k)
-
-        xfb = keep.tile([P, NODE_BLOCKS, H], F32, name="xfb")
-        summed_t = None
-
-        for step in range(H_HALVES * NODE_BLOCKS * CHILDREN):
-            hh = step // (NODE_BLOCKS * CHILDREN)
-            nb = step // CHILDREN % NODE_BLOCKS
-            k = step % CHILDREN
-
-            if k == 0:
-                xf_ps = psum_acc.tile([P, N_TILE], F32, name="acc")
-                mx_product(nc, xf_ps[:], x_codes[:, nb], x_scales[:, nb], w_codes["wf"][:, hh], w_scales["wf"][:, hh])
-                nc.vector.tensor_tensor(out=xfb[:, nb, halves[hh]], in0=xf_ps[:], in1=bias_sb[:, halves[hh]], op=ADD)
-                summed_t = psum_sum.tile([P, BLOCKS, P], F32, name="summed_t")
-
-            hf_ps = psum_acc.tile([P, N_TILE], F32, name="acc")
-            mx_product(nc, hf_ps[:], h_codes[:, nb, k], h_scales[:, nb, k], w_codes["uf"][:, hh], w_scales["uf"][:, hh])
-            z = work.tile([P, N_TILE], F32, name="z")
-            nc.vector.tensor_tensor(out=z[:], in0=hf_ps[:], in1=xfb[:, nb, halves[hh]], op=ADD)
-            gate = work.tile([P, N_TILE], F32, name="gate")
-            nc.scalar.activation(out=gate[:], in_=z[:], func=SIGMOID)
-            weighted = work.tile([P, N_TILE], F32, name="weighted")
-            nc.vector.tensor_tensor(out=weighted[:], in0=gate[:], in1=c_sb[hh, nb][:, k, :], op=MULT)
-
-            for j in range(BLOCKS):
-                nc.tensor.matmul(
-                    out=summed_t[:, j, :],
-                    lhsT=weighted[:, P * j : P * (j + 1)],
-                    rhs=ident[:],
-                    is_transpose=True,
-                    start=(k == 0 and j == 0),
-                    stop=(k == CHILDREN - 1 and j == BLOCKS - 1),
+                nc.tensor.matmul_mx(
+                    out=acc,
+                    lhsT=w_codes[name][:, g, jj, cols].bitcast(FP8X4),
+                    lhsT_scale=w_scales[name][:, g, jj, cols],
+                    rhs=codes[:, g, :].bitcast(FP8X4),
+                    rhs_scale=scales[:, g, :],
+                    start=(g == 0),
+                    stop=(g == PASSES - 1),
                 )
 
-            if k == CHILDREN - 1:
-                summed_t_sb = work.tile([P, BLOCKS, P], F32, name="summed_t_sb")
-                nc.scalar.copy(out=summed_t_sb[:], in_=summed_t[:])
-                result_ps = psum_back.tile([P, N_TILE], F32, name="result_ps")
-                for j in range(BLOCKS):
-                    nc.tensor.transpose(result_ps[:, P * j : P * (j + 1)], summed_t_sb[:, j, :], ident[:])
-                result = work.tile([P, N_TILE], F32, name="result")
-                nc.scalar.copy(out=result[:], in_=result_ps[:])
-                nc.sync.dma_start(out=out[node_rows[nb], halves[hh]], in_=result[:])
+        def prepare_xf(jj):
+            acc = psum_acc.tile([P, N_TILE], F32, name="acc")
+            for e in range(2):
+                product(acc[:, NODES * e : NODES * (e + 1)], "wf", jj, e, x_codes, x_scales)
+            for e in range(2):
+                col = 2 * jj + e
+                nc.scalar.activation(
+                    out=xfb[:, jj, e, :],
+                    in_=acc[:, NODES * e : NODES * (e + 1)],
+                    func=IDENTITY,
+                    bias=bias[:, col : col + 1],
+                )
 
-            child = step + AHEAD
-            if child < NODE_BLOCKS * CHILDREN:
-                prepare_child(child // CHILDREN, child % CHILDREN)
-            if hh == 0 and step % 4 == 3:
-                prepare_weight_pass(("wf", "uf")[step // 8], 1, step // 4 % PASSES)
+        rounds = [
+            (jj, nb, kh) for jj in range(COL_PAIRS) for nb in range(NODE_BLOCKS) for kh in range(PARTS)
+        ]
+        gates = {}
+        cells = {}
+        weighted = {}
+        sums = {}
+
+        accs = {}
+        zs = {}
+
+        def multiply(r, e):
+            jj, nb, kh = rounds[r]
+            accs[r, e] = psum_acc.tile([P, N_TILE], F32, name="acc")
+            product(accs[r, e][:], "uf", jj, e, h_codes[:, nb, kh], h_scales[:, nb, kh])
+
+        def add_shared(r, e):
+            jj, nb, kh = rounds[r]
+            if e == 0:
+                zs[r] = work.tile([P, 2, N_TILE], F32, name="z")
+            shared = xfb[:, jj, e, P * nb : P * (nb + 1)]
+            nc.vector.tensor_tensor(
+                out=zs[r][:, e, :].rearrange("p (k n) -> p k n", k=PART),
+                in0=accs[r, e][:].rearrange("p (k n) -> p k n", k=PART),
+                in1=shared.unsqueeze(1).to_broadcast([P, PART, P]),
+                op=ADD,
+            )
+
+        def gate(r, e):
+            if e == 0:
+                gates[r] = work.tile([P, 2, N_TILE], F32, name="gate")
+            nc.scalar.activation(out=gates[r][:, e, :], in_=zs[r][:, e, :], func=SIGMOID)
+
+        def turn_cells(r):
+            jj, nb, kh = rounds[r]
+            words = c_sb[nb, kh, jj // 2][:].bitcast(F32)
+            cells[r] = psum_cell.tile([P, PART, P], F32, name="cell")
+            for k in range(PART):
+                first = PAIR * k + P * (jj % 2)
+                nc.tensor.transpose(cells[r][:, k, :], words[:, first : first + P], ident[:])
+
+        def weigh(r, e):
+            if e == 0:
+                weighted[r] = work.tile([P, 2, N_TILE], F32, name="weighted")
+            pairs = cells[r][:].rearrange("p k n -> p (k n)").bitcast(BF16).rearrange("p (c e) -> p c e", e=2)
+            nc.vector.tensor_tensor(out=weighted[r][:, e, :], in0=gates[r][:, e, :], in1=pairs[:, :, e], op=MULT)
+
+        def add_up(r, e):
+            jj, nb, kh = rounds[r]
+            if kh == 0 and e == 0:
+                sums[jj, nb] = psum_sum.tile([P, 2, P], F32, name="summed")
+            for k in range(PART):
+                nc.tensor.matmul(
+                    out=sums[jj, nb][:, e, :],
+                    lhsT=weighted[r][:, e, P * k : P * (k + 1)],
+                    rhs=ident[:],
+                    is_transpose=True,
+                    start=(kh == 0 and e == 0 and k == 0),
+                    stop=(kh == PARTS - 1 and e == 1 and k == PART - 1),
+                )
+
+        def store(r):
+            jj, nb, kh = rounds[r]
+            result = work.tile([P, PAIR], F32, name="result")
+            nc.scalar.copy(
+                out=result[:].rearrange("p (w e) -> p w e", e=2), in_=sums[jj, nb][:].rearrange("p e w -> p w e")
+            )
+            nc.sync.dma_start(out=out[node_rows[nb], PAIR * jj : PAIR * (jj + 1)], in_=result[:])
+
+        vector_copy = nc.vector.tensor_copy
+        scalar_copy = nc.scalar.copy
+        group_weight("wf", 0, 0, vector_copy)
+        group_weight("wf", 0, 1, scalar_copy)
+        for g in range(PASSES):
+            turn_x(g)
+        for g in range(PASSES):
+            quantise_x(g)
+        quantise_weight("wf", 0, 0)
+        prepare_bias()
+        for g in range(PASSES):
+            turn_children(0, g, 0)
+        for g in range(PASSES):
+            group_weight("uf", 0, g, vector_copy)
+        quantise_weight("wf", 0, 1)
+        prepare_xf(0)
+        for g in range(PASSES):
+            quantise_weight("uf", 0, g)
+        for g in range(PASSES):
+            turn_children(0, g, 1)
+        for g in range(PASSES):
+            quantise_children(0, g)
+
+        sets = NODE_BLOCKS * PARTS
+
+        def turn_half_set(i):
+            if i < PASSES * (sets - 1):
+                for half in range(2):
+                    turn_children(i // PASSES + 1, i % PASSES, half)
+
+        def quantise_half_set(i):
+            if i < PASSES * (sets - 1):
+                quantise_children(i // PASSES + 1, i % PASSES)
+
+        def piece(i):
+            return ("wf", "uf")[i // PASSES % 2], 1 + i // (2 * PASSES), i % PASSES
+
+        copies = {1: ((0, scalar_copy), (1, vector_copy)), 2: ((2, scalar_copy), (3, vector_copy))}
+        for i in range(4, 12):
+            copies[i - 1] = ((i, scalar_copy),)
+
+        for r in range(len(rounds) + 2):
+            if r < len(rounds):
+                for e in range(2):
+                    multiply(r, e)
+                for e in range(2):
+                    add_shared(r, e)
+            if r == 0:
+                turn_half_set(0)
+                quantise_half_set(0)
+            else:
+                quantise_half_set(2 * r)
+            for i, engine in copies.get(r - 1, ()):
+                quantise_weight(*piece(i))
+            turn_half_set(2 * r + 1)
+            quantise_half_set(2 * r + 1)
+            if r < len(rounds):
+                for e in range(2):
+                    gate(r, e)
+                turn_cells(r)
+            if 0 < r <= len(rounds):
+                for e in range(2):
+                    weigh(r - 1, e)
+            if r > 1:
+                for e in range(2):
+                    add_up(r - 2, e)
+                if rounds[r - 2][2] == PARTS - 1:
+                    store(r - 2)
+            turn_half_set(2 * r + 2)
+            for i, engine in copies.get(r, ()):
+                group_weight(*piece(i), engine)
+            if r in (3, 6, 10):
+                prepare_xf((r + 2) // 4 if r > 3 else 1)

@@ -40,9 +40,9 @@ def tile_childsumtreelstmcell_pa_kernel(tc, x, child_h, child_c, Wf, bWf, Uf, bU
         keep = stack.enter_context(tc.tile_pool(name="keep", bufs=1))
         stage = stack.enter_context(tc.tile_pool(name="stage", bufs=3))
         work = stack.enter_context(tc.tile_pool(name="work", bufs=3))
-        psum_turn = stack.enter_context(tc.psum_pool(name="psum_turn", bufs=2))
+        psum_turn = stack.enter_context(tc.psum_pool(name="psum_turn", bufs=3))
         psum_acc = stack.enter_context(tc.psum_pool(name="psum_acc", bufs=3))
-        psum_cell = stack.enter_context(tc.psum_pool(name="psum_cell", bufs=2))
+        psum_cell = stack.enter_context(tc.psum_pool(name="psum_cell", bufs=1))
         psum_sum = stack.enter_context(tc.psum_pool(name="psum_sum", bufs=1))
 
         stack.enter_context(tc.manual_schedule())
@@ -94,14 +94,14 @@ def tile_childsumtreelstmcell_pa_kernel(tc, x, child_h, child_c, Wf, bWf, Uf, bU
         )
         for row, vec in ((0, bWf), (COL_PAIRS, bUf)):
             nc.sync.dma_start(out=bias_rows[row : row + COL_PAIRS, :], in_=vec.rearrange("(j c) -> j c", c=PAIR))
-        load_weight("wf", Wf, 0, 1)
         load_children(0, 0, 0, 2)
-        load_weight("uf", Uf, 0, 1)
         load_children(0, 0, 2, 2)
+        load_weight("wf", Wf, 0, 1)
+        load_weight("uf", Uf, 0, 1)
         load_children(0, 1, 0, 4)
         load_cells(0, 0, 0)
-        load_children(1, 0, 0, 4)
         load_weight("wf", Wf, 1, 1)
+        load_children(1, 0, 0, 4)
         load_cells(0, 1, 0)
         load_weight("uf", Uf, 1, 1)
         load_children(1, 1, 0, 4)
@@ -123,13 +123,13 @@ def tile_childsumtreelstmcell_pa_kernel(tc, x, child_h, child_c, Wf, bWf, Uf, bU
         h_codes = keep.tile([P, NODE_BLOCKS, PARTS, PASSES, N_TILE], U32, name="h_codes", align_bytes=64)
         h_scales = keep.tile([P, NODE_BLOCKS, PARTS, PASSES, N_TILE], U8, name="h_scales", align_bytes=64)
 
-        def turn_rows(words, first_row, g, grouped):
+        def turn_rows(words, first_row, g, grouped, copy=nc.scalar.copy):
             turned = psum_turn.tile([P, 2, 2, P], F32, name="turned")
             for r in range(2):
                 start = D // 2 * (first_row + r) + PASS_WORDS * g
                 for u in range(2):
                     nc.tensor.transpose(turned[:, r, u, :], words[:, start + u : start + PASS_WORDS : 2], ident[:])
-            nc.scalar.copy(
+            copy(
                 out=grouped.bitcast(F32).rearrange("p (r n u) -> p r n u", r=2, u=2),
                 in_=turned[:].rearrange("p r u n -> p r n u"),
             )
@@ -145,12 +145,12 @@ def tile_childsumtreelstmcell_pa_kernel(tc, x, child_h, child_c, Wf, bWf, Uf, bU
                 out=x_codes[:, g, :].bitcast(FP8X4), scales=x_scales[:, g, :], in_=grouped["x", g][:]
             )
 
-        def turn_children(n, g, half):
+        def turn_children(n, g, half, copy=nc.scalar.copy):
             if half == 0:
                 grouped[n, g] = stage.tile([P, N_TILE * PACK], BF16, name="h_grouped", align_bytes=64)
             size = N_TILE * PACK // 2
             turn_rows(
-                h_sb[n // PARTS, n % PARTS][:].bitcast(F32), 2 * half, g, grouped[n, g][:, size * half : size * (half + 1)]
+                h_sb[n // PARTS, n % PARTS][:].bitcast(F32), 2 * half, g, grouped[n, g][:, size * half : size * (half + 1)], copy
             )
 
         def quantise_children(n, g):
@@ -170,6 +170,7 @@ def tile_childsumtreelstmcell_pa_kernel(tc, x, child_h, child_c, Wf, bWf, Uf, bU
                 in_=grouped[name, jj, g][:].rearrange("p e w t -> p (e w t)"),
             )
 
+        bias_parts = []
         bias = keep.tile([P, 2 * COL_PAIRS], F32, name="bias")
 
         def prepare_bias():
@@ -177,10 +178,14 @@ def tile_childsumtreelstmcell_pa_kernel(tc, x, child_h, child_c, Wf, bWf, Uf, bU
             nc.tensor.transpose(turned[:, 0, 0, :], bias_rows[:].bitcast(F32), ident[:])
             pairs = keep.tile([P, 2 * COL_PAIRS], F32, name="bias_pairs")
             nc.scalar.copy(out=pairs[:], in_=turned[:, 0, 0, 0 : 2 * COL_PAIRS])
-            both = pairs[:].bitcast(BF16)
+            bias_parts.append(pairs[:].bitcast(BF16))
+
+        def add_bias():
+            both = bias_parts[0]
             nc.vector.tensor_tensor(
                 out=bias[:], in0=both[:, 0 : 2 * COL_PAIRS], in1=both[:, 2 * COL_PAIRS : 4 * COL_PAIRS], op=ADD
             )
+
 
         xfb = keep.tile([P, COL_PAIRS, 2, NODES], F32, name="xfb")
 
@@ -281,33 +286,33 @@ def tile_childsumtreelstmcell_pa_kernel(tc, x, child_h, child_c, Wf, bWf, Uf, bU
 
         vector_copy = nc.vector.tensor_copy
         scalar_copy = nc.scalar.copy
-        group_weight("wf", 0, 0, vector_copy)
-        group_weight("wf", 0, 1, scalar_copy)
         for g in range(PASSES):
             turn_x(g)
+        prepare_bias()
         for g in range(PASSES):
             quantise_x(g)
-        quantise_weight("wf", 0, 0)
-        prepare_bias()
         for g in range(PASSES):
             turn_children(0, g, 0)
         for g in range(PASSES):
-            group_weight("uf", 0, g, vector_copy)
-        quantise_weight("wf", 0, 1)
+            turn_children(0, g, 1)
+        add_bias()
+        for g in range(PASSES):
+            group_weight("wf", 0, g, vector_copy)
+        for g in range(PASSES):
+            quantise_weight("wf", 0, g)
         prepare_xf(0)
         for g in range(PASSES):
-            quantise_weight("uf", 0, g)
+            group_weight("uf", 0, g, vector_copy)
         for g in range(PASSES):
-            turn_children(0, g, 1)
+            quantise_weight("uf", 0, g)
         for g in range(PASSES):
             quantise_children(0, g)
 
         sets = NODE_BLOCKS * PARTS
 
-        def turn_half_set(i):
+        def turn_half_set(i, half, copy=nc.scalar.copy):
             if i < PASSES * (sets - 1):
-                for half in range(2):
-                    turn_children(i // PASSES + 1, i % PASSES, half)
+                turn_children(i // PASSES + 1, i % PASSES, half, copy)
 
         def quantise_half_set(i):
             if i < PASSES * (sets - 1):
@@ -316,39 +321,56 @@ def tile_childsumtreelstmcell_pa_kernel(tc, x, child_h, child_c, Wf, bWf, Uf, bU
         def piece(i):
             return ("wf", "uf")[i // PASSES % 2], 1 + i // (2 * PASSES), i % PASSES
 
-        copies = {1: ((0, scalar_copy), (1, vector_copy)), 2: ((2, scalar_copy), (3, vector_copy))}
+        copies = {0: ((0, vector_copy),), 1: ((1, vector_copy), (2, vector_copy)), 2: ((3, vector_copy),)}
         for i in range(4, 12):
-            copies[i - 1] = ((i, scalar_copy),)
+            copies[i - 2] = copies.get(i - 2, ()) + ((i, scalar_copy),)
+        xfs = {3: 1, 6: 2, 10: 3}
+        quants = {}
+        for r, items in copies.items():
+            for i, engine in items:
+                quants.setdefault(r + (1 if i < 4 else 2), []).append(i)
 
         for r in range(len(rounds) + 2):
-            if r < len(rounds):
+            live = r < len(rounds)
+            if live:
                 for e in range(2):
                     multiply(r, e)
+            if r in xfs:
+                prepare_xf(xfs[r])
+            if live:
                 for e in range(2):
                     add_shared(r, e)
+            if 0 < r <= len(rounds):
+                turn_cells(r - 1)
             if r == 0:
-                turn_half_set(0)
+                for i in range(2):
+                    for half in range(2):
+                        turn_half_set(i, half, scalar_copy)
                 quantise_half_set(0)
             else:
                 quantise_half_set(2 * r)
-            for i, engine in copies.get(r - 1, ()):
-                quantise_weight(*piece(i))
-            turn_half_set(2 * r + 1)
-            quantise_half_set(2 * r + 1)
-            if r < len(rounds):
+                for half in range(2):
+                    turn_half_set(2 * r + 1, half)
+            if live:
                 for e in range(2):
                     gate(r, e)
-                turn_cells(r)
+            for i, engine in copies.get(r, ()):
+                if i < 4:
+                    group_weight(*piece(i), engine)
+            for i in quants.get(r, ()):
+                quantise_weight(*piece(i))
+            quantise_half_set(2 * r + 1)
             if 0 < r <= len(rounds):
                 for e in range(2):
                     weigh(r - 1, e)
+
             if r > 1:
                 for e in range(2):
                     add_up(r - 2, e)
                 if rounds[r - 2][2] == PARTS - 1:
                     store(r - 2)
-            turn_half_set(2 * r + 2)
+            for half in range(2):
+                turn_half_set(2 * r + 2, half)
             for i, engine in copies.get(r, ()):
-                group_weight(*piece(i), engine)
-            if r in (3, 6, 10):
-                prepare_xf((r + 2) // 4 if r > 3 else 1)
+                if i >= 4:
+                    group_weight(*piece(i), engine)

@@ -161,7 +161,12 @@ def tile_childsumtreelstmcell_pa_kernel(tc, x, child_h, child_c, Wf, bWf, Uf, bU
 
         def group_weight(name, jj, g, copy):
             grouped[name, jj, g] = stage.tile([P, 2, P, PACK], BF16, name="w_grouped", align_bytes=64)
-            copy(out=grouped[name, jj, g][:], in_=w_raw[name, jj, g].rearrange("p t (w e) -> p e w t", e=2))
+            source = w_raw[name, jj, g].rearrange("p t (w i e) -> p e w t i", i=4, e=2)
+            for e in range(2):
+                copy(
+                    out=grouped[name, jj, g][:, e].rearrange("p (w i) t -> p w t i", i=4),
+                    in_=source[:, e],
+                )
 
         def quantise_weight(name, jj, g):
             nc.vector.quantize_mx(

@@ -28,6 +28,7 @@ PARTS = CHILDREN // PART
 N_TILE = PART * P
 PAIR = 2 * P
 COL_PAIRS = H // PAIR
+TURNING = NODE_BLOCKS * PARTS - 1
 
 FLOPS = 2 * (NODES + NODES * CHILDREN) * D * H
 
@@ -123,13 +124,13 @@ def tile_childsumtreelstmcell_pa_kernel(tc, x, child_h, child_c, Wf, bWf, Uf, bU
         h_codes = keep.tile([P, NODE_BLOCKS, PARTS, PASSES, N_TILE], U32, name="h_codes", align_bytes=64)
         h_scales = keep.tile([P, NODE_BLOCKS, PARTS, PASSES, N_TILE], U8, name="h_scales", align_bytes=64)
 
-        def turn_rows(words, first_row, g, grouped, copy=nc.scalar.copy):
+        def turn_rows(words, first_row, g, grouped):
             turned = psum_turn.tile([P, 2, 2, P], F32, name="turned")
             for r in range(2):
                 start = D // 2 * (first_row + r) + PASS_WORDS * g
                 for u in range(2):
                     nc.tensor.transpose(turned[:, r, u, :], words[:, start + u : start + PASS_WORDS : 2], ident[:])
-            copy(
+            nc.scalar.copy(
                 out=grouped.bitcast(F32).rearrange("p (r n u) -> p r n u", r=2, u=2),
                 in_=turned[:].rearrange("p r u n -> p r n u"),
             )
@@ -145,13 +146,17 @@ def tile_childsumtreelstmcell_pa_kernel(tc, x, child_h, child_c, Wf, bWf, Uf, bU
                 out=x_codes[:, g, :].bitcast(FP8X4), scales=x_scales[:, g, :], in_=grouped["x", g][:]
             )
 
-        def turn_children(n, g, half, copy=nc.scalar.copy):
-            if half == 0:
-                grouped[n, g] = stage.tile([P, N_TILE * PACK], BF16, name="h_grouped", align_bytes=64)
+        def turn_children(n, g, halves=range(2)):
             size = N_TILE * PACK // 2
-            turn_rows(
-                h_sb[n // PARTS, n % PARTS][:].bitcast(F32), 2 * half, g, grouped[n, g][:, size * half : size * (half + 1)], copy
-            )
+            for half in halves:
+                if half == 0:
+                    grouped[n, g] = stage.tile([P, N_TILE * PACK], BF16, name="h_grouped", align_bytes=64)
+                turn_rows(
+                    h_sb[n // PARTS, n % PARTS][:].bitcast(F32),
+                    2 * half,
+                    g,
+                    grouped[n, g][:, size * half : size * (half + 1)],
+                )
 
         def quantise_children(n, g):
             nb, kh = n // PARTS, n % PARTS
@@ -190,7 +195,6 @@ def tile_childsumtreelstmcell_pa_kernel(tc, x, child_h, child_c, Wf, bWf, Uf, bU
             nc.vector.tensor_tensor(
                 out=bias[:], in0=both[:, 0 : 2 * COL_PAIRS], in1=both[:, 2 * COL_PAIRS : 4 * COL_PAIRS], op=ADD
             )
-
 
         xfb = keep.tile([P, COL_PAIRS, 2, NODES], F32, name="xfb")
 
@@ -256,7 +260,10 @@ def tile_childsumtreelstmcell_pa_kernel(tc, x, child_h, child_c, Wf, bWf, Uf, bU
         def turn_cells(r):
             jj, nb, kh = rounds[r]
             words = c_sb[nb, kh, jj // 2][:].bitcast(F32)
-            cells[r] = psum_cell.tile([P, PART, P], F32, name="cell")
+            if r < TURNING:
+                cells[r] = psum_cell.tile([P, PART, P], F32, name="cell")
+            else:
+                cells[r] = psum_turn.tile([P, PART, P], F32, name="turned")
             for k in range(PART):
                 first = PAIR * k + P * (jj % 2)
                 nc.tensor.transpose(cells[r][:, k, :], words[:, first : first + P], ident[:])
@@ -270,7 +277,10 @@ def tile_childsumtreelstmcell_pa_kernel(tc, x, child_h, child_c, Wf, bWf, Uf, bU
         def add_up(r, e):
             jj, nb, kh = rounds[r]
             if kh == 0 and e == 0:
-                sums[jj, nb] = psum_sum.tile([P, 2, P], F32, name="summed")
+                if r >= 6 and r // 2 % 2:
+                    sums[jj, nb] = psum_cell.tile([P, 2, P], F32, name="cell")
+                else:
+                    sums[jj, nb] = psum_sum.tile([P, 2, P], F32, name="summed")
             for k in range(PART):
                 nc.tensor.matmul(
                     out=sums[jj, nb][:, e, :],
@@ -283,99 +293,86 @@ def tile_childsumtreelstmcell_pa_kernel(tc, x, child_h, child_c, Wf, bWf, Uf, bU
 
         def store(r):
             jj, nb, kh = rounds[r]
+            if kh < PARTS - 1:
+                return
             result = work.tile([P, PAIR], F32, name="result")
             nc.scalar.copy(
                 out=result[:].rearrange("p (w e) -> p w e", e=2), in_=sums[jj, nb][:].rearrange("p e w -> p w e")
             )
             nc.sync.dma_start(out=out[node_rows[nb], PAIR * jj : PAIR * (jj + 1)], in_=result[:])
 
-        vector_copy = nc.vector.tensor_copy
-        scalar_copy = nc.scalar.copy
         for g in range(PASSES):
             turn_x(g)
         prepare_bias()
         for g in range(PASSES):
             quantise_x(g)
-        for g in range(PASSES):
-            turn_children(0, g, 0)
-        for g in range(PASSES):
-            turn_children(0, g, 1)
+        for half in range(2):
+            for g in range(PASSES):
+                turn_children(0, g, (half,))
         add_bias()
         for g in range(PASSES):
-            group_weight("wf", 0, g, vector_copy)
+            group_weight("wf", 0, g, nc.vector.tensor_copy)
         for g in range(PASSES):
             quantise_weight("wf", 0, g)
         prepare_xf(0)
         for g in range(PASSES):
-            group_weight("uf", 0, g, vector_copy)
+            group_weight("uf", 0, g, nc.vector.tensor_copy)
         for g in range(PASSES):
             quantise_weight("uf", 0, g)
         for g in range(PASSES):
             quantise_children(0, g)
 
-        sets = NODE_BLOCKS * PARTS
+        pieces = [
+            (name, jj, g) for jj in range(1, COL_PAIRS) for name in ("wf", "uf") for g in range(PASSES)
+        ]
+        early = {0: pieces[0:1], 1: pieces[1:3], 2: pieces[3:4]}
+        LATE = 4
 
-        def turn_half_set(i, half, copy=nc.scalar.copy):
-            if i < PASSES * (sets - 1):
-                turn_children(i // PASSES + 1, i % PASSES, half, copy)
-
-        def quantise_half_set(i):
-            if i < PASSES * (sets - 1):
-                quantise_children(i // PASSES + 1, i % PASSES)
-
-        def piece(i):
-            return ("wf", "uf")[i // PASSES % 2], 1 + i // (2 * PASSES), i % PASSES
-
-        copies = {0: ((0, vector_copy),), 1: ((1, vector_copy), (2, vector_copy)), 2: ((3, vector_copy),)}
-        for i in range(4, 12):
-            copies[i - 2] = copies.get(i - 2, ()) + ((i, scalar_copy),)
-        xfs = {3: 1, 6: 2, 10: 3}
-        quants = {}
-        for r, items in copies.items():
-            for i, engine in items:
-                quants.setdefault(r + (1 if i < 4 else 2), []).append(i)
-
-        for r in range(len(rounds) + 2):
+        for r in range(len(rounds) + 1):
             live = r < len(rounds)
             if live:
-                for e in range(2):
-                    multiply(r, e)
-            if r in xfs:
-                prepare_xf(xfs[r])
-            if live:
-                for e in range(2):
-                    add_shared(r, e)
-            if 0 < r <= len(rounds):
+                multiply(r, 0)
+                add_shared(r, 0)
+                if r == 0:
+                    turn_children(1, 0)
+                multiply(r, 1)
+                if (r + 2) % 4 == 0 and 1 <= (r + 2) // 4 < COL_PAIRS:
+                    prepare_xf((r + 2) // 4)
+                if r > TURNING:
+                    turn_cells(r)
+                add_shared(r, 1)
+            if 0 < r <= TURNING:
                 turn_cells(r - 1)
+            if 0 < r < TURNING:
+                quantise_children(r + 1, 0)
+            if r < TURNING:
+                turn_children(r + 1, 1)
             if r == 0:
-                for i in range(2):
-                    for half in range(2):
-                        turn_half_set(i, half, scalar_copy)
-                quantise_half_set(0)
-            else:
-                quantise_half_set(2 * r)
-                for half in range(2):
-                    turn_half_set(2 * r + 1, half)
+                quantise_children(1, 0)
             if live:
                 for e in range(2):
                     gate(r, e)
-            for i, engine in copies.get(r, ()):
-                if i < 4:
-                    group_weight(*piece(i), engine)
-            for i in quants.get(r, ()):
-                quantise_weight(*piece(i))
-            quantise_half_set(2 * r + 1)
-            if 0 < r <= len(rounds):
+            if LATE <= r < len(pieces):
+                quantise_weight(*pieces[r])
+            if r > 0:
                 for e in range(2):
                     weigh(r - 1, e)
-
+            for piece in early.get(r, ()):
+                group_weight(*piece, nc.vector.tensor_copy)
+            if r < TURNING:
+                quantise_children(r + 1, 1)
+            for piece in early.get(r, ()):
+                quantise_weight(*piece)
+            if r == TURNING:
+                turn_cells(r)
             if r > 1:
                 for e in range(2):
                     add_up(r - 2, e)
-                if rounds[r - 2][2] == PARTS - 1:
-                    store(r - 2)
-            for half in range(2):
-                turn_half_set(2 * r + 2, half)
-            for i, engine in copies.get(r, ()):
-                if i >= 4:
-                    group_weight(*piece(i), engine)
+                store(r - 2)
+            if r + 1 < TURNING:
+                turn_children(r + 2, 0)
+            if LATE <= r + 2 < len(pieces):
+                group_weight(*pieces[r + 2], nc.scalar.copy)
+        for e in range(2):
+            add_up(len(rounds) - 1, e)
+        store(len(rounds) - 1)

@@ -28,7 +28,7 @@ PARTS = CHILDREN // PART
 N_TILE = PART * P
 PAIR = 2 * P
 COL_PAIRS = H // PAIR
-TURNING = NODE_BLOCKS * PARTS - 1
+TURNING = 5
 
 FLOPS = 2 * (NODES + NODES * CHILDREN) * D * H
 
@@ -41,10 +41,10 @@ def tile_childsumtreelstmcell_pa_kernel(tc, x, child_h, child_c, Wf, bWf, Uf, bU
         keep = stack.enter_context(tc.tile_pool(name="keep", bufs=1))
         stage = stack.enter_context(tc.tile_pool(name="stage", bufs=3))
         work = stack.enter_context(tc.tile_pool(name="work", bufs=3))
-        psum_turn = stack.enter_context(tc.psum_pool(name="psum_turn", bufs=3))
+        psum_turn = stack.enter_context(tc.psum_pool(name="psum_turn", bufs=2))
         psum_acc = stack.enter_context(tc.psum_pool(name="psum_acc", bufs=3))
         psum_cell = stack.enter_context(tc.psum_pool(name="psum_cell", bufs=1))
-        psum_sum = stack.enter_context(tc.psum_pool(name="psum_sum", bufs=1))
+        psum_sum = stack.enter_context(tc.psum_pool(name="psum_sum", bufs=2))
 
         stack.enter_context(tc.manual_schedule())
 
@@ -99,17 +99,17 @@ def tile_childsumtreelstmcell_pa_kernel(tc, x, child_h, child_c, Wf, bWf, Uf, bU
         load_children(0, 0, 2, 2)
         load_weight("wf", Wf, 0, 1)
         load_weight("uf", Uf, 0, 1)
-        load_children(0, 1, 0, 4)
-        load_cells(0, 0, 0)
         load_weight("wf", Wf, 1, 1)
-        load_children(1, 0, 0, 4)
-        load_cells(0, 1, 0)
         load_weight("uf", Uf, 1, 1)
+        load_cells(0, 0, 0)
+        load_children(0, 1, 0, 4)
+        load_cells(0, 1, 0)
+        load_children(1, 0, 0, 4)
+        load_weight("wf", Wf, 2, 2)
         load_children(1, 1, 0, 4)
         load_cells(1, 0, 0)
-        load_cells(1, 1, 0)
-        load_weight("wf", Wf, 2, 2)
         load_weight("uf", Uf, 2, 2)
+        load_cells(1, 1, 0)
         for nb in range(NODE_BLOCKS):
             for kh in range(PARTS):
                 load_cells(nb, kh, 1)
@@ -224,9 +224,8 @@ def tile_childsumtreelstmcell_pa_kernel(tc, x, child_h, child_c, Wf, bWf, Uf, bU
                     bias=bias[:, col : col + 1],
                 )
 
-        rounds = [
-            (jj, nb, kh) for jj in range(COL_PAIRS) for nb in range(NODE_BLOCKS) for kh in range(PARTS)
-        ]
+        rounds = [(jj, s // PARTS, s % PARTS) for s in range(NODE_BLOCKS * PARTS) for jj in range(2)]
+        rounds += [(jj, s // PARTS, s % PARTS) for jj in range(2, COL_PAIRS) for s in range(NODE_BLOCKS * PARTS)]
         gates = {}
         cells = {}
         weighted = {}
@@ -272,15 +271,17 @@ def tile_childsumtreelstmcell_pa_kernel(tc, x, child_h, child_c, Wf, bWf, Uf, bU
             if e == 0:
                 weighted[r] = work.tile([P, 2, N_TILE], F32, name="weighted")
             pairs = cells[r][:].rearrange("p k n -> p (k n)").bitcast(BF16).rearrange("p (c e) -> p c e", e=2)
-            nc.vector.tensor_tensor(out=weighted[r][:, e, :], in0=gates[r][:, e, :], in1=pairs[:, :, e], op=MULT)
+            if r < TURNING or r >= len(rounds) - 2:
+                nc.vector.tensor_tensor(out=weighted[r][:, e, :], in0=gates[r][:, e, :], in1=pairs[:, :, e], op=MULT)
+            elif e == 1:
+                nc.vector.tensor_tensor(
+                    out=weighted[r][:], in0=gates[r][:], in1=pairs.rearrange("p c e -> p e c"), op=MULT
+                )
 
         def add_up(r, e):
             jj, nb, kh = rounds[r]
             if kh == 0 and e == 0:
-                if r >= 6 and r // 2 % 2:
-                    sums[jj, nb] = psum_cell.tile([P, 2, P], F32, name="cell")
-                else:
-                    sums[jj, nb] = psum_sum.tile([P, 2, P], F32, name="summed")
+                sums[jj, nb] = psum_sum.tile([P, 2, P], F32, name="summed")
             for k in range(PART):
                 nc.tensor.matmul(
                     out=sums[jj, nb][:, e, :],
@@ -322,57 +323,66 @@ def tile_childsumtreelstmcell_pa_kernel(tc, x, child_h, child_c, Wf, bWf, Uf, bU
         for g in range(PASSES):
             quantise_children(0, g)
 
-        pieces = [
-            (name, jj, g) for jj in range(1, COL_PAIRS) for name in ("wf", "uf") for g in range(PASSES)
-        ]
-        early = {0: pieces[0:1], 1: pieces[1:3], 2: pieces[3:4]}
-        LATE = 4
+        half_sets = [(n, g) for n in range(1, NODE_BLOCKS * PARTS) for g in range(PASSES)]
+        pieces = [(name, jj, g) for jj in range(2, COL_PAIRS) for name in ("wf", "uf") for g in range(PASSES)]
 
+        def turn(i, halves=range(2)):
+            turn_children(*half_sets[i], halves)
+
+        for g in range(PASSES):
+            group_weight("wf", 1, g, nc.vector.tensor_copy)
+        for g in range(PASSES):
+            quantise_weight("wf", 1, g)
         for r in range(len(rounds) + 1):
             live = r < len(rounds)
             if live:
                 multiply(r, 0)
                 add_shared(r, 0)
-                if r == 0:
-                    turn_children(1, 0)
+                if 2 <= r <= TURNING:
+                    quantise_children(*half_sets[r])
+                if r == 1:
+                    turn(1)
+                elif 2 <= r < TURNING:
+                    turn(r + 1, (0,))
                 multiply(r, 1)
-                if (r + 2) % 4 == 0 and 1 <= (r + 2) // 4 < COL_PAIRS:
-                    prepare_xf((r + 2) // 4)
                 if r > TURNING:
                     turn_cells(r)
                 add_shared(r, 1)
-            if 0 < r <= TURNING:
-                turn_cells(r - 1)
-            if 0 < r < TURNING:
-                quantise_children(r + 1, 0)
-            if r < TURNING:
-                turn_children(r + 1, 1)
+                if 2 <= r < TURNING:
+                    turn(r + 1, (1,))
             if r == 0:
-                quantise_children(1, 0)
+                for g, copy in enumerate((nc.vector.tensor_copy, nc.scalar.copy)):
+                    group_weight("uf", 1, g, copy)
+                for g in range(PASSES):
+                    quantise_weight("uf", 1, g)
+                turn(0)
+                prepare_xf(1)
+            elif r <= TURNING:
+                turn_cells(r - 1)
+            if r == 1:
+                quantise_children(*half_sets[0])
             if live:
                 for e in range(2):
                     gate(r, e)
-            if LATE <= r < len(pieces):
-                quantise_weight(*pieces[r])
+            if r == 1:
+                quantise_children(*half_sets[1])
+            if 0 <= r - 4 < len(pieces):
+                quantise_weight(*pieces[r - 4])
             if r > 0:
                 for e in range(2):
                     weigh(r - 1, e)
-            for piece in early.get(r, ()):
-                group_weight(*piece, nc.vector.tensor_copy)
-            if r < TURNING:
-                quantise_children(r + 1, 1)
-            for piece in early.get(r, ()):
-                quantise_weight(*piece)
-            if r == TURNING:
-                turn_cells(r)
+            if r in (6, 10):
+                prepare_xf(2 + (r - 6) // 4)
             if r > 1:
                 for e in range(2):
                     add_up(r - 2, e)
                 store(r - 2)
-            if r + 1 < TURNING:
-                turn_children(r + 2, 0)
-            if LATE <= r + 2 < len(pieces):
-                group_weight(*pieces[r + 2], nc.scalar.copy)
+            if r == TURNING:
+                turn_cells(r)
+            if r == 1:
+                turn(2)
+            if 0 <= r - 2 < len(pieces):
+                group_weight(*pieces[r - 2], nc.scalar.copy)
         for e in range(2):
             add_up(len(rounds) - 1, e)
         store(len(rounds) - 1)

@@ -254,7 +254,10 @@ def tile_childsumtreelstmcell_pa_kernel(tc, x, child_h, child_c, Wf, bWf, Uf, bU
         def gate(r, e):
             if e == 0:
                 gates[r] = work.tile([P, 2, N_TILE], F32, name="gate")
-            nc.scalar.activation(out=gates[r][:, e, :], in_=zs[r][:, e, :], func=SIGMOID)
+            if r <= TURNING or r >= len(rounds) - 2:
+                nc.scalar.activation(out=gates[r][:, e, :], in_=zs[r][:, e, :], func=SIGMOID)
+            elif e == 1:
+                nc.scalar.activation(out=gates[r][:], in_=zs[r][:], func=SIGMOID)
 
         def turn_cells(r):
             jj, nb, kh = rounds[r]
@@ -326,6 +329,9 @@ def tile_childsumtreelstmcell_pa_kernel(tc, x, child_h, child_c, Wf, bWf, Uf, bU
         half_sets = [(n, g) for n in range(1, NODE_BLOCKS * PARTS) for g in range(PASSES)]
         pieces = [(name, jj, g) for jj in range(2, COL_PAIRS) for name in ("wf", "uf") for g in range(PASSES)]
 
+        def gpsimd_copy(out, in_):
+            nc.gpsimd.tensor_scalar(out=out, in0=in_, scalar1=1.0, scalar2=0.0, op0=MULT, op1=ADD)
+
         def turn(i, halves=range(2)):
             turn_children(*half_sets[i], halves)
 
@@ -382,7 +388,7 @@ def tile_childsumtreelstmcell_pa_kernel(tc, x, child_h, child_c, Wf, bWf, Uf, bU
             if r == 1:
                 turn(2)
             if 0 <= r - 2 < len(pieces):
-                group_weight(*pieces[r - 2], nc.scalar.copy)
+                group_weight(*pieces[r - 2], gpsimd_copy if r % 2 == 1 else nc.scalar.copy)
         for e in range(2):
             add_up(len(rounds) - 1, e)
         store(len(rounds) - 1)

@@ -101,8 +101,8 @@ def tile_childsumtreelstmcell_pa_kernel(tc, x, child_h, child_c, Wf, bWf, Uf, bU
         load_weight("uf", Uf, 0, 1)
         load_weight("wf", Wf, 1, 1)
         load_weight("uf", Uf, 1, 1)
-        load_cells(0, 0, 0)
         load_children(0, 1, 0, 4)
+        load_cells(0, 0, 0)
         load_cells(0, 1, 0)
         load_children(1, 0, 0, 4)
         load_weight("wf", Wf, 2, 2)
@@ -198,18 +198,24 @@ def tile_childsumtreelstmcell_pa_kernel(tc, x, child_h, child_c, Wf, bWf, Uf, bU
 
         xfb = keep.tile([P, COL_PAIRS, 2, NODES], F32, name="xfb")
 
-        def product(acc, name, jj, e, codes, scales):
+        def mx_pass(acc, name, jj, e, g, codes, scales, start, stop):
             cols = slice(P * e, P * (e + 1))
+            nc.tensor.matmul_mx(
+                out=acc,
+                lhsT=w_codes[name][:, g, jj, cols].bitcast(FP8X4),
+                lhsT_scale=w_scales[name][:, g, jj, cols],
+                rhs=codes.bitcast(FP8X4),
+                rhs_scale=scales,
+                start=start,
+                stop=stop,
+            )
+
+        def product(acc, name, jj, e, codes, scales):
             for g in range(PASSES):
-                nc.tensor.matmul_mx(
-                    out=acc,
-                    lhsT=w_codes[name][:, g, jj, cols].bitcast(FP8X4),
-                    lhsT_scale=w_scales[name][:, g, jj, cols],
-                    rhs=codes[:, g, :].bitcast(FP8X4),
-                    rhs_scale=scales[:, g, :],
-                    start=(g == 0),
-                    stop=(g == PASSES - 1),
-                )
+                mx_pass(acc, name, jj, e, g, codes[:, g, :], scales[:, g, :], g == 0, g == PASSES - 1)
+
+        def direct(r, e):
+            return r >= len(rounds) - 2 and e == 1
 
         def prepare_xf(jj):
             acc = psum_acc.tile([P, N_TILE], F32, name="acc")
@@ -237,11 +243,23 @@ def tile_childsumtreelstmcell_pa_kernel(tc, x, child_h, child_c, Wf, bWf, Uf, bU
         def multiply(r, e):
             jj, nb, kh = rounds[r]
             accs[r, e] = psum_acc.tile([P, N_TILE], F32, name="acc")
-            product(accs[r, e][:], "uf", jj, e, h_codes[:, nb, kh], h_scales[:, nb, kh])
+            if not direct(r, e):
+                product(accs[r, e][:], "uf", jj, e, h_codes[:, nb, kh], h_scales[:, nb, kh])
+                return
+            codes, scales = h_codes[:, nb, kh], h_scales[:, nb, kh]
+            nodes = slice(P * nb, P * (nb + 1))
+            mx_pass(accs[r, e][:], "uf", jj, e, 0, codes[:, 0, :], scales[:, 0, :], True, False)
+            for g in range(PASSES):
+                for k in range(PART):
+                    part = accs[r, e][:, P * k : P * (k + 1)]
+                    mx_pass(part, "wf", jj, e, g, x_codes[:, g, nodes], x_scales[:, g, nodes], False, False)
+            mx_pass(accs[r, e][:], "uf", jj, e, 1, codes[:, 1, :], scales[:, 1, :], False, True)
 
         def add_shared(r, e):
+            if direct(r, e):
+                return
             jj, nb, kh = rounds[r]
-            if e == 0:
+            if r not in zs:
                 zs[r] = work.tile([P, 2, N_TILE], F32, name="z")
             shared = xfb[:, jj, e, P * nb : P * (nb + 1)]
             nc.vector.tensor_tensor(
@@ -254,7 +272,12 @@ def tile_childsumtreelstmcell_pa_kernel(tc, x, child_h, child_c, Wf, bWf, Uf, bU
         def gate(r, e):
             if e == 0:
                 gates[r] = work.tile([P, 2, N_TILE], F32, name="gate")
-            if r <= TURNING or r >= len(rounds) - 2:
+            if direct(r, e):
+                col = 2 * rounds[r][0] + e
+                nc.scalar.activation(
+                    out=gates[r][:, e, :], in_=accs[r, e][:], func=SIGMOID, bias=bias[:, col : col + 1]
+                )
+            elif r <= TURNING or r >= len(rounds) - 2:
                 nc.scalar.activation(out=gates[r][:, e, :], in_=zs[r][:, e, :], func=SIGMOID)
             elif e == 1:
                 nc.scalar.activation(out=gates[r][:], in_=zs[r][:], func=SIGMOID)
@@ -281,18 +304,30 @@ def tile_childsumtreelstmcell_pa_kernel(tc, x, child_h, child_c, Wf, bWf, Uf, bU
                     out=weighted[r][:], in0=gates[r][:], in1=pairs.rearrange("p c e -> p e c"), op=MULT
                 )
 
+        def folds(r):
+            return 11 <= r < 14
+
+        folded = {}
+
+        def fold(r):
+            folded[r] = work.tile([P, 2, PAIR], F32, name="folded")
+            nc.gpsimd.tensor_tensor(
+                out=folded[r][:], in0=weighted[r][:, :, 0:PAIR], in1=weighted[r][:, :, PAIR : 2 * PAIR], op=ADD
+            )
+
         def add_up(r, e):
             jj, nb, kh = rounds[r]
             if kh == 0 and e == 0:
                 sums[jj, nb] = psum_sum.tile([P, 2, P], F32, name="summed")
-            for k in range(PART):
+            source, count = (folded[r], PART // 2) if folds(r) else (weighted[r], PART)
+            for k in range(count):
                 nc.tensor.matmul(
                     out=sums[jj, nb][:, e, :],
-                    lhsT=weighted[r][:, e, P * k : P * (k + 1)],
+                    lhsT=source[:, e, P * k : P * (k + 1)],
                     rhs=ident[:],
                     is_transpose=True,
                     start=(kh == 0 and e == 0 and k == 0),
-                    stop=(kh == PARTS - 1 and e == 1 and k == PART - 1),
+                    stop=(kh == PARTS - 1 and e == 1 and k == count - 1),
                 )
 
         def store(r):
@@ -346,9 +381,7 @@ def tile_childsumtreelstmcell_pa_kernel(tc, x, child_h, child_c, Wf, bWf, Uf, bU
                 add_shared(r, 0)
                 if 2 <= r <= TURNING:
                     quantise_children(*half_sets[r])
-                if r == 1:
-                    turn(1)
-                elif 2 <= r < TURNING:
+                if 2 <= r < TURNING:
                     turn(r + 1, (0,))
                 multiply(r, 1)
                 if r > TURNING:
@@ -357,15 +390,16 @@ def tile_childsumtreelstmcell_pa_kernel(tc, x, child_h, child_c, Wf, bWf, Uf, bU
                 if 2 <= r < TURNING:
                     turn(r + 1, (1,))
             if r == 0:
-                for g, copy in enumerate((nc.vector.tensor_copy, nc.scalar.copy)):
-                    group_weight("uf", 1, g, copy)
+                for g in range(PASSES):
+                    group_weight("uf", 1, g, nc.vector.tensor_copy)
                 for g in range(PASSES):
                     quantise_weight("uf", 1, g)
                 turn(0)
+                turn(1)
                 prepare_xf(1)
             elif r <= TURNING:
                 turn_cells(r - 1)
-            if r == 1:
+            if r == 0:
                 quantise_children(*half_sets[0])
             if live:
                 for e in range(2):
@@ -377,12 +411,15 @@ def tile_childsumtreelstmcell_pa_kernel(tc, x, child_h, child_c, Wf, bWf, Uf, bU
             if r > 0:
                 for e in range(2):
                     weigh(r - 1, e)
+                if folds(r - 1):
+                    fold(r - 1)
             if r in (6, 10):
                 prepare_xf(2 + (r - 6) // 4)
-            if r > 1:
-                for e in range(2):
-                    add_up(r - 2, e)
-                store(r - 2)
+            for done in (r - 3, r - 2):
+                if 0 <= done and folds(done) == (done == r - 3):
+                    for e in range(2):
+                        add_up(done, e)
+                    store(done)
             if r == TURNING:
                 turn_cells(r)
             if r == 1:

@@ -117,8 +117,8 @@ def tile_childsumtreelstmcell_pa_kernel(tc, x, child_h, child_c, Wf, bWf, Uf, bU
         w_codes = {}
         w_scales = {}
         for name in ("wf", "uf"):
-            w_codes[name] = keep.tile([P, PASSES, COL_PAIRS, PAIR], U32, name=name + "_codes", align_bytes=64)
-            w_scales[name] = keep.tile([P, PASSES, COL_PAIRS, PAIR], U8, name=name + "_scales", align_bytes=64)
+            w_codes[name] = keep.tile([P, COL_PAIRS, PASSES, PAIR], U32, name=name + "_codes", align_bytes=64)
+            w_scales[name] = keep.tile([P, COL_PAIRS, PASSES, PAIR], U8, name=name + "_scales", align_bytes=64)
         x_codes = keep.tile([P, PASSES, NODES], U32, name="x_codes", align_bytes=64)
         x_scales = keep.tile([P, PASSES, NODES], U8, name="x_scales", align_bytes=64)
         h_codes = keep.tile([P, NODE_BLOCKS, PARTS, PASSES, N_TILE], U32, name="h_codes", align_bytes=64)
@@ -165,19 +165,20 @@ def tile_childsumtreelstmcell_pa_kernel(tc, x, child_h, child_c, Wf, bWf, Uf, bU
             )
 
         def group_weight(name, jj, g, copy):
-            grouped[name, jj, g] = stage.tile([P, 2, P, PACK], BF16, name="w_grouped", align_bytes=64)
+            if g == 0:
+                grouped[name, jj] = stage.tile([P, PASSES, 2, P, PACK], BF16, name="w_grouped", align_bytes=64)
             source = w_raw[name, jj, g].rearrange("p t (w i e) -> p e w t i", i=4, e=2)
             for e in range(2):
                 copy(
-                    out=grouped[name, jj, g][:, e].rearrange("p (w i) t -> p w t i", i=4),
+                    out=grouped[name, jj][:, g, e].rearrange("p (w i) t -> p w t i", i=4),
                     in_=source[:, e],
                 )
 
-        def quantise_weight(name, jj, g):
+        def quantise_weight(name, jj, passes):
             nc.vector.quantize_mx(
-                out=w_codes[name][:, g, jj, :].bitcast(FP8X4),
-                scales=w_scales[name][:, g, jj, :],
-                in_=grouped[name, jj, g][:].rearrange("p e w t -> p (e w t)"),
+                out=w_codes[name][:, jj, passes].rearrange("p g c -> p (g c)").bitcast(FP8X4),
+                scales=w_scales[name][:, jj, passes].rearrange("p g c -> p (g c)"),
+                in_=grouped[name, jj][:, passes].rearrange("p g e w t -> p (g e w t)"),
             )
 
         bias_parts = []
@@ -202,8 +203,8 @@ def tile_childsumtreelstmcell_pa_kernel(tc, x, child_h, child_c, Wf, bWf, Uf, bU
             cols = slice(P * e, P * (e + 1))
             nc.tensor.matmul_mx(
                 out=acc,
-                lhsT=w_codes[name][:, g, jj, cols].bitcast(FP8X4),
-                lhsT_scale=w_scales[name][:, g, jj, cols],
+                lhsT=w_codes[name][:, jj, g, cols].bitcast(FP8X4),
+                lhsT_scale=w_scales[name][:, jj, g, cols],
                 rhs=codes.bitcast(FP8X4),
                 rhs_scale=scales,
                 start=start,
@@ -305,7 +306,7 @@ def tile_childsumtreelstmcell_pa_kernel(tc, x, child_h, child_c, Wf, bWf, Uf, bU
                 )
 
         def folds(r):
-            return 11 <= r < 14
+            return 8 <= r < 14
 
         folded = {}
 
@@ -352,17 +353,17 @@ def tile_childsumtreelstmcell_pa_kernel(tc, x, child_h, child_c, Wf, bWf, Uf, bU
         for g in range(PASSES):
             group_weight("wf", 0, g, nc.vector.tensor_copy)
         for g in range(PASSES):
-            quantise_weight("wf", 0, g)
+            quantise_weight("wf", 0, slice(g, g + 1))
         prepare_xf(0)
         for g in range(PASSES):
             group_weight("uf", 0, g, nc.vector.tensor_copy)
         for g in range(PASSES):
-            quantise_weight("uf", 0, g)
+            quantise_weight("uf", 0, slice(g, g + 1))
         for g in range(PASSES):
             quantise_children(0, g)
 
         half_sets = [(n, g) for n in range(1, NODE_BLOCKS * PARTS) for g in range(PASSES)]
-        pieces = [(name, jj, g) for jj in range(2, COL_PAIRS) for name in ("wf", "uf") for g in range(PASSES)]
+        pieces = [("wf", 2), ("wf", 3), ("uf", 2), ("uf", 3)]
 
         def gpsimd_copy(out, in_):
             nc.gpsimd.tensor_scalar(out=out, in0=in_, scalar1=1.0, scalar2=0.0, op0=MULT, op1=ADD)
@@ -370,10 +371,10 @@ def tile_childsumtreelstmcell_pa_kernel(tc, x, child_h, child_c, Wf, bWf, Uf, bU
         def turn(i, halves=range(2)):
             turn_children(*half_sets[i], halves)
 
+        group_weight("wf", 1, 0, nc.vector.tensor_copy)
+        group_weight("wf", 1, 1, nc.scalar.copy)
         for g in range(PASSES):
-            group_weight("wf", 1, g, nc.vector.tensor_copy)
-        for g in range(PASSES):
-            quantise_weight("wf", 1, g)
+            quantise_weight("wf", 1, slice(g, g + 1))
         for r in range(len(rounds) + 1):
             live = r < len(rounds)
             if live:
@@ -393,7 +394,7 @@ def tile_childsumtreelstmcell_pa_kernel(tc, x, child_h, child_c, Wf, bWf, Uf, bU
                 for g in range(PASSES):
                     group_weight("uf", 1, g, nc.vector.tensor_copy)
                 for g in range(PASSES):
-                    quantise_weight("uf", 1, g)
+                    quantise_weight("uf", 1, slice(g, g + 1))
                 turn(0)
                 turn(1)
                 prepare_xf(1)
@@ -407,14 +408,14 @@ def tile_childsumtreelstmcell_pa_kernel(tc, x, child_h, child_c, Wf, bWf, Uf, bU
             if r == 1:
                 quantise_children(*half_sets[1])
             if 0 <= r - 4 < len(pieces):
-                quantise_weight(*pieces[r - 4])
+                quantise_weight(*pieces[r - 4], slice(0, PASSES))
             if r > 0:
                 for e in range(2):
                     weigh(r - 1, e)
                 if folds(r - 1):
                     fold(r - 1)
-            if r in (6, 10):
-                prepare_xf(2 + (r - 6) // 4)
+            if r in (6, 7):
+                prepare_xf(2 if r == 6 else 3)
             for done in (r - 3, r - 2):
                 if 0 <= done and folds(done) == (done == r - 3):
                     for e in range(2):
@@ -425,7 +426,8 @@ def tile_childsumtreelstmcell_pa_kernel(tc, x, child_h, child_c, Wf, bWf, Uf, bU
             if r == 1:
                 turn(2)
             if 0 <= r - 2 < len(pieces):
-                group_weight(*pieces[r - 2], gpsimd_copy if r % 2 == 1 else nc.scalar.copy)
+                for g, copy in enumerate((nc.scalar.copy, gpsimd_copy)):
+                    group_weight(*pieces[r - 2], g, copy)
         for e in range(2):
             add_up(len(rounds) - 1, e)
         store(len(rounds) - 1)

@@ -41,9 +41,8 @@ def tile_childsumtreelstmcell_pa_kernel(tc, x, child_h, child_c, Wf, bWf, Uf, bU
         keep = stack.enter_context(tc.tile_pool(name="keep", bufs=1))
         stage = stack.enter_context(tc.tile_pool(name="stage", bufs=3))
         work = stack.enter_context(tc.tile_pool(name="work", bufs=3))
-        psum_turn = stack.enter_context(tc.psum_pool(name="psum_turn", bufs=2))
+        psum_turn = stack.enter_context(tc.psum_pool(name="psum_turn", bufs=3))
         psum_acc = stack.enter_context(tc.psum_pool(name="psum_acc", bufs=3))
-        psum_cell = stack.enter_context(tc.psum_pool(name="psum_cell", bufs=1))
         psum_sum = stack.enter_context(tc.psum_pool(name="psum_sum", bufs=2))
 
         stack.enter_context(tc.manual_schedule())
@@ -286,10 +285,7 @@ def tile_childsumtreelstmcell_pa_kernel(tc, x, child_h, child_c, Wf, bWf, Uf, bU
         def turn_cells(r):
             jj, nb, kh = rounds[r]
             words = c_sb[nb, kh, jj // 2][:].bitcast(F32)
-            if r < TURNING:
-                cells[r] = psum_cell.tile([P, PART, P], F32, name="cell")
-            else:
-                cells[r] = psum_turn.tile([P, PART, P], F32, name="turned")
+            cells[r] = psum_turn.tile([P, PART, P], F32, name="turned")
             for k in range(PART):
                 first = PAIR * k + P * (jj % 2)
                 nc.tensor.transpose(cells[r][:, k, :], words[:, first : first + P], ident[:])

@@ -92,15 +92,15 @@ def tile_childsumtreelstmcell_pa_kernel(tc, x, child_h, child_c, Wf, bWf, Uf, bU
             out=x_sb[:].rearrange("p (b d) -> p b d", b=NODE_BLOCKS),
             in_=x.rearrange("(b p) d -> p b d", p=P),
         )
-        for row, vec in ((0, bWf), (COL_PAIRS, bUf)):
-            nc.sync.dma_start(out=bias_rows[row : row + COL_PAIRS, :], in_=vec.rearrange("(j c) -> j c", c=PAIR))
+        load_weight("wf", Wf, 0, 1)
         load_children(0, 0, 0, 2)
         load_children(0, 0, 2, 2)
-        load_weight("wf", Wf, 0, 1)
+        for row, vec in ((0, bWf), (COL_PAIRS, bUf)):
+            nc.sync.dma_start(out=bias_rows[row : row + COL_PAIRS, :], in_=vec.rearrange("(j c) -> j c", c=PAIR))
         load_weight("uf", Uf, 0, 1)
+        load_children(0, 1, 0, 4)
         load_weight("wf", Wf, 1, 1)
         load_weight("uf", Uf, 1, 1)
-        load_children(0, 1, 0, 4)
         load_cells(0, 0, 0)
         load_cells(0, 1, 0)
         load_children(1, 0, 0, 4)
@@ -339,24 +339,25 @@ def tile_childsumtreelstmcell_pa_kernel(tc, x, child_h, child_c, Wf, bWf, Uf, bU
 
         for g in range(PASSES):
             turn_x(g)
-        prepare_bias()
-        for g in range(PASSES):
-            quantise_x(g)
-        for half in range(2):
-            for g in range(PASSES):
-                turn_children(0, g, (half,))
-        add_bias()
         for g in range(PASSES):
             group_weight("wf", 0, g, nc.vector.tensor_copy)
         for g in range(PASSES):
+            quantise_x(g)
+        for g in range(PASSES):
             quantise_weight("wf", 0, slice(g, g + 1))
-        prepare_xf(0)
+        for half in range(2):
+            for g in range(PASSES):
+                turn_children(0, g, (half,))
+            if half == 0:
+                prepare_bias()
+                add_bias()
         for g in range(PASSES):
             group_weight("uf", 0, g, nc.vector.tensor_copy)
-        for g in range(PASSES):
-            quantise_weight("uf", 0, slice(g, g + 1))
+        prepare_xf(0)
         for g in range(PASSES):
             quantise_children(0, g)
+        for g in range(PASSES):
+            quantise_weight("uf", 0, slice(g, g + 1))
 
         half_sets = [(n, g) for n in range(1, NODE_BLOCKS * PARTS) for g in range(PASSES)]
         pieces = [("wf", 2), ("wf", 3), ("uf", 2), ("uf", 3)]
@@ -367,11 +368,25 @@ def tile_childsumtreelstmcell_pa_kernel(tc, x, child_h, child_c, Wf, bWf, Uf, bU
         def turn(i, halves=range(2)):
             turn_children(*half_sets[i], halves)
 
-        group_weight("wf", 1, 0, nc.vector.tensor_copy)
-        group_weight("wf", 1, 1, nc.scalar.copy)
+        turn(0)
+        multiply(0, 0)
+        multiply(0, 1)
+        for g in range(PASSES):
+            group_weight("wf", 1, g, nc.vector.tensor_copy)
         for g in range(PASSES):
             quantise_weight("wf", 1, slice(g, g + 1))
-        for r in range(len(rounds) + 1):
+        add_shared(0, 0)
+        add_shared(0, 1)
+        turn(1)
+        for g in range(PASSES):
+            group_weight("uf", 1, g, nc.vector.tensor_copy)
+        gate(0, 0)
+        gate(0, 1)
+        for g in range(PASSES):
+            quantise_weight("uf", 1, slice(g, g + 1))
+        prepare_xf(1)
+        quantise_children(*half_sets[0])
+        for r in range(1, len(rounds) + 1):
             live = r < len(rounds)
             if live:
                 multiply(r, 0)
@@ -386,18 +401,10 @@ def tile_childsumtreelstmcell_pa_kernel(tc, x, child_h, child_c, Wf, bWf, Uf, bU
                 add_shared(r, 1)
                 if 2 <= r < TURNING:
                     turn(r + 1, (1,))
-            if r == 0:
-                for g in range(PASSES):
-                    group_weight("uf", 1, g, nc.vector.tensor_copy)
-                for g in range(PASSES):
-                    quantise_weight("uf", 1, slice(g, g + 1))
-                turn(0)
-                turn(1)
-                prepare_xf(1)
-            elif r <= TURNING:
+            if r <= TURNING:
                 turn_cells(r - 1)
-            if r == 0:
-                quantise_children(*half_sets[0])
+            if r in (6, 7):
+                prepare_xf(2 if r == 6 else 3)
             if live:
                 for e in range(2):
                     gate(r, e)
@@ -410,8 +417,6 @@ def tile_childsumtreelstmcell_pa_kernel(tc, x, child_h, child_c, Wf, bWf, Uf, bU
                     weigh(r - 1, e)
                 if folds(r - 1):
                     fold(r - 1)
-            if r in (6, 7):
-                prepare_xf(2 if r == 6 else 3)
             for done in (r - 3, r - 2):
                 if 0 <= done and folds(done) == (done == r - 3):
                     for e in range(2):

@@ -53,6 +53,14 @@ def tile_childsumtreelstmcell_pa_kernel(tc, x, child_h, child_c, Wf, bWf, Uf, bU
         make_identity(nc, ident[:])
         bias_rows = const.tile([P, PAIR], BF16, name="bias_rows")
         nc.vector.memset(bias_rows[:], 0.0)
+        blank = const.tile([P, N_TILE], BF16, name="blank")
+        nc.vector.memset(blank[:], 0.0)
+
+        def keep_clock(count):
+            bank = psum_acc.tile([P, N_TILE], F32, name="acc")
+            for i in range(count):
+                nc.tensor.matmul(out=bank[:], lhsT=blank[:, 0:P], rhs=blank[:], start=True, stop=True)
+
         warm = const.tile([P, 1], F32, name="warm")
         nc.scalar.activation(out=warm[:], in_=ident[:, 0:1], func=SIGMOID)
 
@@ -102,8 +110,8 @@ def tile_childsumtreelstmcell_pa_kernel(tc, x, child_h, child_c, Wf, bWf, Uf, bU
         load_weight("wf", Wf, 1, 1)
         load_weight("uf", Uf, 1, 1)
         load_cells(0, 0, 0)
-        load_cells(0, 1, 0)
         load_children(1, 0, 0, 4)
+        load_cells(0, 1, 0)
         load_weight("wf", Wf, 2, 2)
         load_children(1, 1, 0, 4)
         load_cells(1, 0, 0)
@@ -354,6 +362,7 @@ def tile_childsumtreelstmcell_pa_kernel(tc, x, child_h, child_c, Wf, bWf, Uf, bU
         for g in range(PASSES):
             group_weight("uf", 0, g, nc.vector.tensor_copy)
         prepare_xf(0)
+        keep_clock(2)
         for g in range(PASSES):
             quantise_children(0, g)
         for g in range(PASSES):
@@ -377,14 +386,14 @@ def tile_childsumtreelstmcell_pa_kernel(tc, x, child_h, child_c, Wf, bWf, Uf, bU
             quantise_weight("wf", 1, slice(g, g + 1))
         add_shared(0, 0)
         add_shared(0, 1)
+        group_weight("uf", 1, 0, nc.scalar.copy)
         turn(1)
-        for g in range(PASSES):
-            group_weight("uf", 1, g, nc.vector.tensor_copy)
-        gate(0, 0)
-        gate(0, 1)
+        group_weight("uf", 1, 1, nc.vector.tensor_copy)
         for g in range(PASSES):
             quantise_weight("uf", 1, slice(g, g + 1))
         prepare_xf(1)
+        gate(0, 0)
+        gate(0, 1)
         quantise_children(*half_sets[0])
         for r in range(1, len(rounds) + 1):
             live = r < len(rounds)
@@ -395,16 +404,18 @@ def tile_childsumtreelstmcell_pa_kernel(tc, x, child_h, child_c, Wf, bWf, Uf, bU
                     quantise_children(*half_sets[r])
                 if 2 <= r < TURNING:
                     turn(r + 1, (0,))
+                if 2 <= r <= TURNING:
+                    turn_cells(r - 1)
                 multiply(r, 1)
+                if r in (6, 7):
+                    prepare_xf(2 if r == 6 else 3)
                 if r > TURNING:
                     turn_cells(r)
                 add_shared(r, 1)
                 if 2 <= r < TURNING:
                     turn(r + 1, (1,))
-            if r <= TURNING:
-                turn_cells(r - 1)
-            if r in (6, 7):
-                prepare_xf(2 if r == 6 else 3)
+            if r == 1:
+                turn_cells(0)
             if live:
                 for e in range(2):
                     gate(r, e)

@@ -100,26 +100,28 @@ def tile_childsumtreelstmcell_pa_kernel(tc, x, child_h, child_c, Wf, bWf, Uf, bU
             out=x_sb[:].rearrange("p (b d) -> p b d", b=NODE_BLOCKS),
             in_=x.rearrange("(b p) d -> p b d", p=P),
         )
-        load_weight("wf", Wf, 0, 1)
+        load_weight("wf", Wf, 0, 2)
         load_children(0, 0, 0, 2)
         load_children(0, 0, 2, 2)
         for row, vec in ((0, bWf), (COL_PAIRS, bUf)):
             nc.sync.dma_start(out=bias_rows[row : row + COL_PAIRS, :], in_=vec.rearrange("(j c) -> j c", c=PAIR))
         load_weight("uf", Uf, 0, 1)
         load_children(0, 1, 0, 4)
-        load_weight("wf", Wf, 1, 1)
         load_weight("uf", Uf, 1, 1)
         load_cells(0, 0, 0)
         load_children(1, 0, 0, 4)
         load_cells(0, 1, 0)
-        load_weight("wf", Wf, 2, 2)
         load_children(1, 1, 0, 4)
+        load_weight("wf", Wf, 2, 1)
         load_cells(1, 0, 0)
-        load_weight("uf", Uf, 2, 2)
+        load_weight("uf", Uf, 2, 1)
         load_cells(1, 1, 0)
-        for nb in range(NODE_BLOCKS):
-            for kh in range(PARTS):
-                load_cells(nb, kh, 1)
+        load_cells(0, 0, 1)
+        load_cells(0, 1, 1)
+        load_weight("wf", Wf, 3, 1)
+        load_weight("uf", Uf, 3, 1)
+        load_cells(1, 0, 1)
+        load_cells(1, 1, 1)
 
         w_codes = {}
         w_scales = {}
@@ -369,10 +371,13 @@ def tile_childsumtreelstmcell_pa_kernel(tc, x, child_h, child_c, Wf, bWf, Uf, bU
             quantise_weight("uf", 0, slice(g, g + 1))
 
         half_sets = [(n, g) for n in range(1, NODE_BLOCKS * PARTS) for g in range(PASSES)]
+        V, S = nc.vector.tensor_copy, nc.scalar.copy
         pieces = [("wf", 2), ("wf", 3), ("uf", 2), ("uf", 3)]
 
         def gpsimd_copy(out, in_):
             nc.gpsimd.tensor_scalar(out=out, in0=in_, scalar1=1.0, scalar2=0.0, op0=MULT, op1=ADD)
+
+        G = gpsimd_copy
 
         def turn(i, halves=range(2)):
             turn_children(*half_sets[i], halves)
@@ -407,8 +412,8 @@ def tile_childsumtreelstmcell_pa_kernel(tc, x, child_h, child_c, Wf, bWf, Uf, bU
                 if 2 <= r <= TURNING:
                     turn_cells(r - 1)
                 multiply(r, 1)
-                if r in (6, 7):
-                    prepare_xf(2 if r == 6 else 3)
+                if r in {6: 2, 8: 3}:
+                    prepare_xf({6: 2, 8: 3}[r])
                 if r > TURNING:
                     turn_cells(r)
                 add_shared(r, 1)
@@ -421,8 +426,8 @@ def tile_childsumtreelstmcell_pa_kernel(tc, x, child_h, child_c, Wf, bWf, Uf, bU
                     gate(r, e)
             if r == 1:
                 quantise_children(*half_sets[1])
-            if 0 <= r - 4 < len(pieces):
-                quantise_weight(*pieces[r - 4], slice(0, PASSES))
+            for i in {5:(0,),6:(2,),7:(1,),9:(3,)}.get(r, ()):
+                quantise_weight(*pieces[i], slice(0, PASSES))
             if r > 0:
                 for e in range(2):
                     weigh(r - 1, e)
@@ -437,9 +442,8 @@ def tile_childsumtreelstmcell_pa_kernel(tc, x, child_h, child_c, Wf, bWf, Uf, bU
                 turn_cells(r)
             if r == 1:
                 turn(2)
-            if 0 <= r - 2 < len(pieces):
-                for g, copy in enumerate((nc.scalar.copy, gpsimd_copy)):
-                    group_weight(*pieces[r - 2], g, copy)
+            for i, g, copy in {3:((0,0,S),(0,1,G)), 4:((2,0,S),(2,1,G)), 5:((1,0,S),(1,1,S)), 6:((3,0,S),),7:((3,1,S),)}.get(r, ()):
+                group_weight(*pieces[i], g, copy)
         for e in range(2):
             add_up(len(rounds) - 1, e)
         store(len(rounds) - 1)

@@ -53,14 +53,6 @@ def tile_childsumtreelstmcell_pa_kernel(tc, x, child_h, child_c, Wf, bWf, Uf, bU
         make_identity(nc, ident[:])
         bias_rows = const.tile([P, PAIR], BF16, name="bias_rows")
         nc.vector.memset(bias_rows[:], 0.0)
-        blank = const.tile([P, N_TILE], BF16, name="blank")
-        nc.vector.memset(blank[:], 0.0)
-
-        def keep_clock(count):
-            bank = psum_acc.tile([P, N_TILE], F32, name="acc")
-            for i in range(count):
-                nc.tensor.matmul(out=bank[:], lhsT=blank[:, 0:P], rhs=blank[:], start=True, stop=True)
-
         warm = const.tile([P, 1], F32, name="warm")
         nc.scalar.activation(out=warm[:], in_=ident[:, 0:1], func=SIGMOID)
 
@@ -109,7 +101,8 @@ def tile_childsumtreelstmcell_pa_kernel(tc, x, child_h, child_c, Wf, bWf, Uf, bU
         load_children(0, 1, 0, 4)
         load_weight("uf", Uf, 1, 1)
         load_cells(0, 0, 0)
-        load_children(1, 0, 0, 4)
+        load_children(1, 0, 0, 2)
+        load_children(1, 0, 2, 2)
         load_cells(0, 1, 0)
         load_children(1, 1, 0, 4)
         load_weight("wf", Wf, 2, 1)
@@ -225,7 +218,7 @@ def tile_childsumtreelstmcell_pa_kernel(tc, x, child_h, child_c, Wf, bWf, Uf, bU
                 mx_pass(acc, name, jj, e, g, codes[:, g, :], scales[:, g, :], g == 0, g == PASSES - 1)
 
         def direct(r, e):
-            return r >= len(rounds) - 2 and e == 1
+            return e == 1 and (r in (10, 13, 15))
 
         def prepare_xf(jj):
             acc = psum_acc.tile([P, N_TILE], F32, name="acc")
@@ -287,7 +280,7 @@ def tile_childsumtreelstmcell_pa_kernel(tc, x, child_h, child_c, Wf, bWf, Uf, bU
                 nc.scalar.activation(
                     out=gates[r][:, e, :], in_=accs[r, e][:], func=SIGMOID, bias=bias[:, col : col + 1]
                 )
-            elif r <= TURNING or r >= len(rounds) - 2:
+            elif r <= TURNING or r >= len(rounds) - 2 or direct(r, 1):
                 nc.scalar.activation(out=gates[r][:, e, :], in_=zs[r][:, e, :], func=SIGMOID)
             elif e == 1:
                 nc.scalar.activation(out=gates[r][:], in_=zs[r][:], func=SIGMOID)
@@ -312,7 +305,7 @@ def tile_childsumtreelstmcell_pa_kernel(tc, x, child_h, child_c, Wf, bWf, Uf, bU
                 )
 
         def folds(r):
-            return 8 <= r < 14
+            return 8 <= r < 13
 
         folded = {}
 
@@ -347,24 +340,27 @@ def tile_childsumtreelstmcell_pa_kernel(tc, x, child_h, child_c, Wf, bWf, Uf, bU
             )
             nc.sync.dma_start(out=out[node_rows[nb], PAIR * jj : PAIR * (jj + 1)], in_=result[:])
 
+        group_weight("wf", 0, 0, nc.vector.tensor_copy)
+        group_weight("wf", 1, 0, nc.scalar.copy)
         for g in range(PASSES):
             turn_x(g)
-        for g in range(PASSES):
-            group_weight("wf", 0, g, nc.vector.tensor_copy)
-        for g in range(PASSES):
-            quantise_x(g)
+        group_weight("wf", 0, 1, nc.vector.tensor_copy)
+        group_weight("wf", 1, 1, nc.scalar.copy)
         for g in range(PASSES):
             quantise_weight("wf", 0, slice(g, g + 1))
+        for g in range(PASSES):
+            quantise_x(g)
+        quantise_weight("wf", 1, slice(0, PASSES))
         for half in range(2):
             for g in range(PASSES):
                 turn_children(0, g, (half,))
             if half == 0:
                 prepare_bias()
-                add_bias()
-        for g in range(PASSES):
-            group_weight("uf", 0, g, nc.vector.tensor_copy)
+        add_bias()
+        group_weight("uf", 0, 0, nc.vector.tensor_copy)
+        group_weight("uf", 0, 1, nc.scalar.copy)
         prepare_xf(0)
-        keep_clock(2)
+        prepare_xf(1)
         for g in range(PASSES):
             quantise_children(0, g)
         for g in range(PASSES):
@@ -382,21 +378,16 @@ def tile_childsumtreelstmcell_pa_kernel(tc, x, child_h, child_c, Wf, bWf, Uf, bU
         def turn(i, halves=range(2)):
             turn_children(*half_sets[i], halves)
 
-        turn(0)
         multiply(0, 0)
         multiply(0, 1)
-        for g in range(PASSES):
-            group_weight("wf", 1, g, nc.vector.tensor_copy)
-        for g in range(PASSES):
-            quantise_weight("wf", 1, slice(g, g + 1))
+        turn(0)
         add_shared(0, 0)
         add_shared(0, 1)
-        group_weight("uf", 1, 0, nc.scalar.copy)
+        for g in range(PASSES):
+            group_weight("uf", 1, g, nc.vector.tensor_copy)
         turn(1)
-        group_weight("uf", 1, 1, nc.vector.tensor_copy)
         for g in range(PASSES):
             quantise_weight("uf", 1, slice(g, g + 1))
-        prepare_xf(1)
         gate(0, 0)
         gate(0, 1)
         quantise_children(*half_sets[0])

@@ -53,6 +53,14 @@ def tile_childsumtreelstmcell_pa_kernel(tc, x, child_h, child_c, Wf, bWf, Uf, bU
         make_identity(nc, ident[:])
         bias_rows = const.tile([P, PAIR], BF16, name="bias_rows")
         nc.vector.memset(bias_rows[:], 0.0)
+        blank = const.tile([P, N_TILE], BF16, name="blank")
+        nc.vector.memset(blank[:], 0.0)
+
+        def keep_clock(count):
+            bank = psum_acc.tile([P, N_TILE], F32, name="acc")
+            for i in range(count):
+                nc.tensor.matmul(out=bank[:], lhsT=blank[:, 0:P], rhs=blank[:], start=True, stop=True)
+
         warm = const.tile([P, 1], F32, name="warm")
         nc.scalar.activation(out=warm[:], in_=ident[:, 0:1], func=SIGMOID)
 
@@ -105,13 +113,12 @@ def tile_childsumtreelstmcell_pa_kernel(tc, x, child_h, child_c, Wf, bWf, Uf, bU
         load_children(1, 0, 2, 2)
         load_cells(0, 1, 0)
         load_children(1, 1, 0, 4)
-        load_weight("wf", Wf, 2, 1)
+        load_weight("wf", Wf, 2, 2)
         load_cells(1, 0, 0)
         load_weight("uf", Uf, 2, 1)
         load_cells(1, 1, 0)
         load_cells(0, 0, 1)
         load_cells(0, 1, 1)
-        load_weight("wf", Wf, 3, 1)
         load_weight("uf", Uf, 3, 1)
         load_cells(1, 0, 1)
         load_cells(1, 1, 1)
@@ -385,6 +392,7 @@ def tile_childsumtreelstmcell_pa_kernel(tc, x, child_h, child_c, Wf, bWf, Uf, bU
         add_shared(0, 1)
         for g in range(PASSES):
             group_weight("uf", 1, g, nc.vector.tensor_copy)
+        keep_clock(2)
         turn(1)
         for g in range(PASSES):
             quantise_weight("uf", 1, slice(g, g + 1))

@@ -108,9 +108,9 @@ def tile_childsumtreelstmcell_pa_kernel(tc, x, child_h, child_c, Wf, bWf, Uf, bU
         load_weight("uf", Uf, 0, 1)
         load_children(0, 1, 0, 4)
         load_weight("uf", Uf, 1, 1)
-        load_cells(0, 0, 0)
         load_children(1, 0, 0, 2)
         load_children(1, 0, 2, 2)
+        load_cells(0, 0, 0)
         load_cells(0, 1, 0)
         load_children(1, 1, 0, 4)
         load_weight("wf", Wf, 2, 2)
@@ -225,7 +225,7 @@ def tile_childsumtreelstmcell_pa_kernel(tc, x, child_h, child_c, Wf, bWf, Uf, bU
                 mx_pass(acc, name, jj, e, g, codes[:, g, :], scales[:, g, :], g == 0, g == PASSES - 1)
 
         def direct(r, e):
-            return e == 1 and (r in (10, 13, 15))
+            return e == 1 and (r in (10, 14, 15))
 
         def prepare_xf(jj):
             acc = psum_acc.tile([P, N_TILE], F32, name="acc")
@@ -312,7 +312,7 @@ def tile_childsumtreelstmcell_pa_kernel(tc, x, child_h, child_c, Wf, bWf, Uf, bU
                 )
 
         def folds(r):
-            return 8 <= r < 13
+            return 8 <= r < 14
 
         folded = {}
 
@@ -419,6 +419,7 @@ def tile_childsumtreelstmcell_pa_kernel(tc, x, child_h, child_c, Wf, bWf, Uf, bU
                 if 2 <= r < TURNING:
                     turn(r + 1, (1,))
             if r == 1:
+                turn(2)
                 turn_cells(0)
             if live:
                 for e in range(2):
@@ -439,8 +440,6 @@ def tile_childsumtreelstmcell_pa_kernel(tc, x, child_h, child_c, Wf, bWf, Uf, bU
                     store(done)
             if r == TURNING:
                 turn_cells(r)
-            if r == 1:
-                turn(2)
             for i, g, copy in {3:((0,0,S),(0,1,G)), 4:((2,0,S),(2,1,G)), 5:((1,0,S),(1,1,S)), 6:((3,0,S),),7:((3,1,S),)}.get(r, ()):
                 group_weight(*pieces[i], g, copy)
         for e in range(2):

from contextlib import ExitStack

import concourse.mybir as mybir
from concourse.masks import make_identity

F32 = mybir.dt.float32
BF16 = mybir.dt.bfloat16
U32 = mybir.dt.uint32
U8 = mybir.dt.uint8
FP8X4 = mybir.dt.float8_e4m3fn_x4
ADD = mybir.AluOpType.add
MULT = mybir.AluOpType.mult
SIGMOID = mybir.ActivationFunctionType.Sigmoid
IDENTITY = mybir.ActivationFunctionType.Identity

P = 128
NODES = 256
CHILDREN = 8
D = 1024
H = 1024
PACK = 4
K_PASS = P * PACK
PASSES = D // K_PASS
PASS_WORDS = K_PASS // 2
NODE_BLOCKS = NODES // P
PART = 4
PARTS = CHILDREN // PART
N_TILE = PART * P
PAIR = 2 * P
COL_PAIRS = H // PAIR
TURNING = 5

FLOPS = 2 * (NODES + NODES * CHILDREN) * D * H


def tile_childsumtreelstmcell_pa_kernel(tc, x, child_h, child_c, Wf, bWf, Uf, bUf, out):
    nc = tc.nc
    with ExitStack() as stack:
        const = stack.enter_context(tc.tile_pool(name="const", bufs=1))
        inputs = stack.enter_context(tc.tile_pool(name="inputs", bufs=1))
        keep = stack.enter_context(tc.tile_pool(name="keep", bufs=1))
        stage = stack.enter_context(tc.tile_pool(name="stage", bufs=3))
        work = stack.enter_context(tc.tile_pool(name="work", bufs=3))
        psum_turn = stack.enter_context(tc.psum_pool(name="psum_turn", bufs=3))
        psum_acc = stack.enter_context(tc.psum_pool(name="psum_acc", bufs=3))
        psum_sum = stack.enter_context(tc.psum_pool(name="psum_sum", bufs=2))

        stack.enter_context(tc.manual_schedule())

        node_rows = [slice(P * nb, P * (nb + 1)) for nb in range(NODE_BLOCKS)]

        ident = const.tile([P, P], F32, name="ident")
        make_identity(nc, ident[:])
        bias_rows = const.tile([P, PAIR], BF16, name="bias_rows")
        nc.vector.memset(bias_rows[:], 0.0)
        blank = const.tile([P, N_TILE], BF16, name="blank")
        nc.vector.memset(blank[:], 0.0)

        def keep_clock(count):
            bank = psum_acc.tile([P, N_TILE], F32, name="acc")
            for i in range(count):
                nc.tensor.matmul(out=bank[:], lhsT=blank[:, 0:P], rhs=blank[:], start=True, stop=True)

        warm = const.tile([P, 1], F32, name="warm")
        nc.scalar.activation(out=warm[:], in_=ident[:, 0:1], func=SIGMOID)

        x_sb = inputs.tile([P, NODE_BLOCKS * D], BF16, name="x_sb")
        h_sb = {}
        c_sb = {}
        w_raw = {}

        def load_weight(name, w, jj, count):
            first, width = PAIR * jj, PAIR * count
            for g in range(PASSES):
                raw = inputs.tile([P, PACK, width], BF16, name="%s_raw%d%d" % (name, jj, g))
                nc.sync.dma_start(
                    out=raw[:],
                    in_=w[K_PASS * g : K_PASS * (g + 1), first : first + width].rearrange("(p t) c -> p t c", t=PACK),
                )
                for i in range(count):
                    w_raw[name, jj + i, g] = raw[:, :, PAIR * i : PAIR * (i + 1)]

        def load_children(nb, kh, first, count):
            if first == 0:
                h_sb[nb, kh] = inputs.tile([P, PART * D], BF16, name="h_sb%d%d" % (nb, kh))
            kids = slice(PART * kh + first, PART * kh + first + count)
            nc.sync.dma_start(
                out=h_sb[nb, kh][:].rearrange("p (k d) -> p k d", k=PART)[:, first : first + count, :],
                in_=child_h[node_rows[nb], kids, :],
            )

        def load_cells(nb, kh, half):
            c_sb[nb, kh, half] = inputs.tile([P, PART * 2 * PAIR], BF16, name="c_sb%d%d%d" % (nb, kh, half))
            nc.sync.dma_start(
                out=c_sb[nb, kh, half][:].rearrange("p (k c) -> p k c", k=PART),
                in_=child_c[node_rows[nb], PART * kh : PART * (kh + 1), 2 * PAIR * half : 2 * PAIR * (half + 1)],
            )

        nc.sync.dma_start(
            out=x_sb[:].rearrange("p (b d) -> p b d", b=NODE_BLOCKS),
            in_=x.rearrange("(b p) d -> p b d", p=P),
        )
        load_weight("wf", Wf, 0, 2)
        load_children(0, 0, 0, 2)
        load_children(0, 0, 2, 2)
        for row, vec in ((0, bWf), (COL_PAIRS, bUf)):
            nc.sync.dma_start(out=bias_rows[row : row + COL_PAIRS, :], in_=vec.rearrange("(j c) -> j c", c=PAIR))
        load_weight("uf", Uf, 0, 1)
        load_children(0, 1, 0, 4)
        load_weight("uf", Uf, 1, 1)
        load_children(1, 0, 0, 2)
        load_children(1, 0, 2, 2)
        load_cells(0, 0, 0)
        load_cells(0, 1, 0)
        load_children(1, 1, 0, 4)
        load_weight("wf", Wf, 2, 2)
        load_cells(1, 0, 0)
        load_weight("uf", Uf, 2, 1)
        load_cells(1, 1, 0)
        load_cells(0, 0, 1)
        load_cells(0, 1, 1)
        load_weight("uf", Uf, 3, 1)
        load_cells(1, 0, 1)
        load_cells(1, 1, 1)

        w_codes = {}
        w_scales = {}
        for name in ("wf", "uf"):
            w_codes[name] = keep.tile([P, COL_PAIRS, PASSES, PAIR], U32, name=name + "_codes", align_bytes=64)
            w_scales[name] = keep.tile([P, COL_PAIRS, PASSES, PAIR], U8, name=name + "_scales", align_bytes=64)
        x_codes = keep.tile([P, PASSES, NODES], U32, name="x_codes", align_bytes=64)
        x_scales = keep.tile([P, PASSES, NODES], U8, name="x_scales", align_bytes=64)
        h_codes = keep.tile([P, NODE_BLOCKS, PARTS, PASSES, N_TILE], U32, name="h_codes", align_bytes=64)
        h_scales = keep.tile([P, NODE_BLOCKS, PARTS, PASSES, N_TILE], U8, name="h_scales", align_bytes=64)

        def turn_rows(words, first_row, g, grouped):
            turned = psum_turn.tile([P, 2, 2, P], F32, name="turned")
            for r in range(2):
                start = D // 2 * (first_row + r) + PASS_WORDS * g
                for u in range(2):
                    nc.tensor.transpose(turned[:, r, u, :], words[:, start + u : start + PASS_WORDS : 2], ident[:])
            nc.scalar.copy(
                out=grouped.bitcast(F32).rearrange("p (r n u) -> p r n u", r=2, u=2),
                in_=turned[:].rearrange("p r u n -> p r n u"),
            )

        grouped = {}

        def turn_x(g):
            grouped["x", g] = stage.tile([P, NODES * PACK], BF16, name="x_grouped", align_bytes=64)
            turn_rows(x_sb[:].bitcast(F32), 0, g, grouped["x", g][:])

        def quantise_x(g):
            nc.vector.quantize_mx(
                out=x_codes[:, g, :].bitcast(FP8X4), scales=x_scales[:, g, :], in_=grouped["x", g][:]
            )

        def turn_children(n, g, halves=range(2)):
            size = N_TILE * PACK // 2
            for half in halves:
                if half == 0:
                    grouped[n, g] = stage.tile([P, N_TILE * PACK], BF16, name="h_grouped", align_bytes=64)
                turn_rows(
                    h_sb[n // PARTS, n % PARTS][:].bitcast(F32),
                    2 * half,
                    g,
                    grouped[n, g][:, size * half : size * (half + 1)],
                )

        def quantise_children(n, g):
            nb, kh = n // PARTS, n % PARTS
            nc.vector.quantize_mx(
                out=h_codes[:, nb, kh, g, :].bitcast(FP8X4), scales=h_scales[:, nb, kh, g, :], in_=grouped[n, g][:]
            )

        def group_weight(name, jj, g, copy):
            if g == 0:
                grouped[name, jj] = stage.tile([P, PASSES, 2, P, PACK], BF16, name="w_grouped", align_bytes=64)
            source = w_raw[name, jj, g].rearrange("p t (w i e) -> p e w t i", i=4, e=2)
            for e in range(2):
                copy(
                    out=grouped[name, jj][:, g, e].rearrange("p (w i) t -> p w t i", i=4),
                    in_=source[:, e],
                )

        def quantise_weight(name, jj, passes):
            nc.vector.quantize_mx(
                out=w_codes[name][:, jj, passes].rearrange("p g c -> p (g c)").bitcast(FP8X4),
                scales=w_scales[name][:, jj, passes].rearrange("p g c -> p (g c)"),
                in_=grouped[name, jj][:, passes].rearrange("p g e w t -> p (g e w t)"),
            )

        bias_parts = []
        bias = keep.tile([P, 2 * COL_PAIRS], F32, name="bias")

        def prepare_bias():
            turned = psum_turn.tile([P, 2, 2, P], F32, name="turned")
            nc.tensor.transpose(turned[:, 0, 0, :], bias_rows[:].bitcast(F32), ident[:])
            pairs = keep.tile([P, 2 * COL_PAIRS], F32, name="bias_pairs")
            nc.scalar.copy(out=pairs[:], in_=turned[:, 0, 0, 0 : 2 * COL_PAIRS])
            bias_parts.append(pairs[:].bitcast(BF16))

        def add_bias():
            both = bias_parts[0]
            nc.vector.tensor_tensor(
                out=bias[:], in0=both[:, 0 : 2 * COL_PAIRS], in1=both[:, 2 * COL_PAIRS : 4 * COL_PAIRS], op=ADD
            )

        xfb = keep.tile([P, COL_PAIRS, 2, NODES], F32, name="xfb")

        def mx_pass(acc, name, jj, e, g, codes, scales, start, stop):
            cols = slice(P * e, P * (e + 1))
            nc.tensor.matmul_mx(
                out=acc,
                lhsT=w_codes[name][:, jj, g, cols].bitcast(FP8X4),
                lhsT_scale=w_scales[name][:, jj, g, cols],
                rhs=codes.bitcast(FP8X4),
                rhs_scale=scales,
                start=start,
                stop=stop,
            )

        def product(acc, name, jj, e, codes, scales):
            for g in range(PASSES):
                mx_pass(acc, name, jj, e, g, codes[:, g, :], scales[:, g, :], g == 0, g == PASSES - 1)

        def direct(r, e):
            return e == 1 and (r in (10, 14, 15))

        def prepare_xf(jj):
            acc = psum_acc.tile([P, N_TILE], F32, name="acc")
            for e in range(2):
                product(acc[:, NODES * e : NODES * (e + 1)], "wf", jj, e, x_codes, x_scales)
            for e in range(2):
                col = 2 * jj + e
                nc.scalar.activation(
                    out=xfb[:, jj, e, :],
                    in_=acc[:, NODES * e : NODES * (e + 1)],
                    func=IDENTITY,
                    bias=bias[:, col : col + 1],
                )

        rounds = [(jj, s // PARTS, s % PARTS) for s in range(NODE_BLOCKS * PARTS) for jj in range(2)]
        rounds += [(jj, s // PARTS, s % PARTS) for jj in range(2, COL_PAIRS) for s in range(NODE_BLOCKS * PARTS)]
        gates = {}
        cells = {}
        weighted = {}
        sums = {}

        accs = {}
        zs = {}

        def multiply(r, e):
            jj, nb, kh = rounds[r]
            accs[r, e] = psum_acc.tile([P, N_TILE], F32, name="acc")
            if not direct(r, e):
                product(accs[r, e][:], "uf", jj, e, h_codes[:, nb, kh], h_scales[:, nb, kh])
                return
            codes, scales = h_codes[:, nb, kh], h_scales[:, nb, kh]
            nodes = slice(P * nb, P * (nb + 1))
            mx_pass(accs[r, e][:], "uf", jj, e, 0, codes[:, 0, :], scales[:, 0, :], True, False)
            for g in range(PASSES):
                for k in range(PART):
                    part = accs[r, e][:, P * k : P * (k + 1)]
                    mx_pass(part, "wf", jj, e, g, x_codes[:, g, nodes], x_scales[:, g, nodes], False, False)
            mx_pass(accs[r, e][:], "uf", jj, e, 1, codes[:, 1, :], scales[:, 1, :], False, True)

        def add_shared(r, e):
            if direct(r, e):
                return
            jj, nb, kh = rounds[r]
            if r not in zs:
                zs[r] = work.tile([P, 2, N_TILE], F32, name="z")
            shared = xfb[:, jj, e, P * nb : P * (nb + 1)]
            nc.vector.tensor_tensor(
                out=zs[r][:, e, :].rearrange("p (k n) -> p k n", k=PART),
                in0=accs[r, e][:].rearrange("p (k n) -> p k n", k=PART),
                in1=shared.unsqueeze(1).to_broadcast([P, PART, P]),
                op=ADD,
            )

        def gate(r, e):
            if e == 0:
                gates[r] = work.tile([P, 2, N_TILE], F32, name="gate")
            if direct(r, e):
                col = 2 * rounds[r][0] + e
                nc.scalar.activation(
                    out=gates[r][:, e, :], in_=accs[r, e][:], func=SIGMOID, bias=bias[:, col : col + 1]
                )
            elif r <= TURNING or r >= len(rounds) - 2 or direct(r, 1):
                nc.scalar.activation(out=gates[r][:, e, :], in_=zs[r][:, e, :], func=SIGMOID)
            elif e == 1:
                nc.scalar.activation(out=gates[r][:], in_=zs[r][:], func=SIGMOID)

        def turn_cells(r):
            jj, nb, kh = rounds[r]
            words = c_sb[nb, kh, jj // 2][:].bitcast(F32)
            cells[r] = psum_turn.tile([P, PART, P], F32, name="turned")
            for k in range(PART):
                first = PAIR * k + P * (jj % 2)
                nc.tensor.transpose(cells[r][:, k, :], words[:, first : first + P], ident[:])

        def weigh(r, e):
            if e == 0:
                weighted[r] = work.tile([P, 2, N_TILE], F32, name="weighted")
            pairs = cells[r][:].rearrange("p k n -> p (k n)").bitcast(BF16).rearrange("p (c e) -> p c e", e=2)
            if r < TURNING or r >= len(rounds) - 2:
                nc.vector.tensor_tensor(out=weighted[r][:, e, :], in0=gates[r][:, e, :], in1=pairs[:, :, e], op=MULT)
            elif e == 1:
                nc.vector.tensor_tensor(
                    out=weighted[r][:], in0=gates[r][:], in1=pairs.rearrange("p c e -> p e c"), op=MULT
                )

        def folds(r):
            return 8 <= r < 14

        folded = {}

        def fold(r):
            folded[r] = work.tile([P, 2, PAIR], F32, name="folded")
            nc.gpsimd.tensor_tensor(
                out=folded[r][:], in0=weighted[r][:, :, 0:PAIR], in1=weighted[r][:, :, PAIR : 2 * PAIR], op=ADD
            )

        def add_up(r, e):
            jj, nb, kh = rounds[r]
            if kh == 0 and e == 0:
                sums[jj, nb] = psum_sum.tile([P, 2, P], F32, name="summed")
            source, count = (folded[r], PART // 2) if folds(r) else (weighted[r], PART)
            for k in range(count):
                nc.tensor.matmul(
                    out=sums[jj, nb][:, e, :],
                    lhsT=source[:, e, P * k : P * (k + 1)],
                    rhs=ident[:],
                    is_transpose=True,
                    start=(kh == 0 and e == 0 and k == 0),
                    stop=(kh == PARTS - 1 and e == 1 and k == count - 1),
                )

        def store(r):
            jj, nb, kh = rounds[r]
            if kh < PARTS - 1:
                return
            result = work.tile([P, PAIR], F32, name="result")
            nc.scalar.copy(
                out=result[:].rearrange("p (w e) -> p w e", e=2), in_=sums[jj, nb][:].rearrange("p e w -> p w e")
            )
            nc.sync.dma_start(out=out[node_rows[nb], PAIR * jj : PAIR * (jj + 1)], in_=result[:])

        group_weight("wf", 0, 0, nc.vector.tensor_copy)
        group_weight("wf", 1, 0, nc.scalar.copy)
        for g in range(PASSES):
            turn_x(g)
        group_weight("wf", 0, 1, nc.vector.tensor_copy)
        group_weight("wf", 1, 1, nc.scalar.copy)
        for g in range(PASSES):
            quantise_weight("wf", 0, slice(g, g + 1))
        for g in range(PASSES):
            quantise_x(g)
        quantise_weight("wf", 1, slice(0, PASSES))
        for half in range(2):
            for g in range(PASSES):
                turn_children(0, g, (half,))
            if half == 0:
                prepare_bias()
        add_bias()
        group_weight("uf", 0, 0, nc.vector.tensor_copy)
        group_weight("uf", 0, 1, nc.scalar.copy)
        prepare_xf(0)
        prepare_xf(1)
        for g in range(PASSES):
            quantise_children(0, g)
        for g in range(PASSES):
            quantise_weight("uf", 0, slice(g, g + 1))

        half_sets = [(n, g) for n in range(1, NODE_BLOCKS * PARTS) for g in range(PASSES)]
        V, S = nc.vector.tensor_copy, nc.scalar.copy
        pieces = [("wf", 2), ("wf", 3), ("uf", 2), ("uf", 3)]

        def gpsimd_copy(out, in_):
            nc.gpsimd.tensor_scalar(out=out, in0=in_, scalar1=1.0, scalar2=0.0, op0=MULT, op1=ADD)

        G = gpsimd_copy

        def turn(i, halves=range(2)):
            turn_children(*half_sets[i], halves)

        multiply(0, 0)
        multiply(0, 1)
        turn(0)
        add_shared(0, 0)
        add_shared(0, 1)
        for g in range(PASSES):
            group_weight("uf", 1, g, nc.vector.tensor_copy)
        keep_clock(2)
        turn(1)
        for g in range(PASSES):
            quantise_weight("uf", 1, slice(g, g + 1))
        gate(0, 0)
        gate(0, 1)
        quantise_children(*half_sets[0])
        for r in range(1, len(rounds) + 1):
            live = r < len(rounds)
            if live:
                multiply(r, 0)
                add_shared(r, 0)
                if 2 <= r <= TURNING:
                    quantise_children(*half_sets[r])
                if 2 <= r < TURNING:
                    turn(r + 1, (0,))
                if 2 <= r <= TURNING:
                    turn_cells(r - 1)
                multiply(r, 1)
                if r in {6: 2, 8: 3}:
                    prepare_xf({6: 2, 8: 3}[r])
                if r > TURNING:
                    turn_cells(r)
                add_shared(r, 1)
                if 2 <= r < TURNING:
                    turn(r + 1, (1,))
            if r == 1:
                turn(2)
                turn_cells(0)
            if live:
                for e in range(2):
                    gate(r, e)
            if r == 1:
                quantise_children(*half_sets[1])
            for i in {5:(0,),6:(2,),7:(1,),9:(3,)}.get(r, ()):
                quantise_weight(*pieces[i], slice(0, PASSES))
            if r > 0:
                for e in range(2):
                    weigh(r - 1, e)
                if folds(r - 1):
                    fold(r - 1)
            for done in (r - 3, r - 2):
                if 0 <= done and folds(done) == (done == r - 3):
                    for e in range(2):
                        add_up(done, e)
                    store(done)
            if r == TURNING:
                turn_cells(r)
            for i, g, copy in {3:((0,0,S),(0,1,G)), 4:((2,0,S),(2,1,G)), 5:((1,0,S),(1,1,S)), 6:((3,0,S),),7:((3,1,S),)}.get(r, ()):
                group_weight(*pieces[i], g, copy)
        for e in range(2):
            add_up(len(rounds) - 1, e)
        store(len(rounds) - 1)
